import numpy as np
import ml_dtypes


def mxq(x, axis, fmt="e4m3"):
    dtype, down = {"e4m3": (ml_dtypes.float8_e4m3fn, 7), "e5m2": (ml_dtypes.float8_e5m2, 14)}[fmt]
    v = np.moveaxis(np.asarray(x, np.float32).astype(ml_dtypes.bfloat16).astype(np.float64), axis, -1)
    blocks = v.reshape(v.shape[:-1] + (-1, 32))
    amax = np.abs(blocks).max(-1, keepdims=True)
    byte = np.maximum(np.where(amax > 0, np.frexp(amax)[1] - 1 + 127, 0) - down, 1)
    scale = np.exp2(byte - 127.0)
    codes = (blocks / scale).astype(np.float32).astype(dtype).astype(np.float64)
    return np.moveaxis((codes * scale).reshape(v.shape), -1, axis)


WIDE = False


def mx_kscale(k):
    if not WIDE:
        return np.ones(k)
    levels = np.array([18, -18])
    if k % 512:
        return np.exp2(np.random.permutation(np.resize(levels, k // 32))).repeat(32)
    a = np.empty((k // 512, 16))
    for p in range(k // 512):
        a[p, :8] = np.random.permutation(np.resize(levels, 8))
        for g in range(8):
            far = levels[np.abs(levels - a[p, g]) >= 10]
            a[p, g + 8] = far[np.random.randint(len(far))]
    return np.exp2(a.ravel()).repeat(32)


BF16 = ml_dtypes.bfloat16


def bf(x):
    return np.asarray(x, np.float32).astype(BF16)


def f64(x):
    return np.asarray(x).astype(np.float64)


B, N, HID, H, D = 1, 1024, 768, 8, 128
T, J = B * N, 3 * H * D


def rope_backward(g, rope):
    gp = g.reshape(g.shape[:-1] + (D // 2, 2))
    rp = rope[:, None].reshape(rope.shape[0], 1, rope.shape[1], D // 2, 2)
    cos, sin = rp[..., 0], rp[..., 1]
    g0, g1 = gp[..., 0], gp[..., 1]
    out = np.stack([g0 * cos + g1 * sin, g1 * cos - g0 * sin], axis=-1)
    return out.reshape(g.shape)


def setup_inputs():
    s = mx_kscale(T).reshape(B, N)
    u = mx_kscale(J)
    st = s[:, None, :, None]
    uh = u.reshape(3, 1, H, 1, D)
    img = bf(np.random.standard_normal((B, N, HID)) * s[:, :, None])
    rope = bf(np.random.standard_normal((B, N, D)))
    w = bf(np.random.standard_normal((J, HID)) / np.sqrt(HID) / u[:, None])
    gs = []
    for i in range(3):
        e = np.exp2(np.random.randint(-6, 1, (B, 1, N, 1)))
        gs.append(bf(np.random.standard_normal((B, H, N, D)) * e / st * uh[i]))
    return {"img": img, "rope": rope, "W_img_qkv": w,
            "grad_0": gs[0], "grad_1": gs[1], "grad_2": gs[2]}


def reference(img, rope, W_img_qkv, grad_0, grad_1, grad_2):
    r = f64(rope)
    dq = rope_backward(f64(grad_0), r)
    dk = rope_backward(f64(grad_1), r)
    dv = f64(grad_2)
    dy = np.stack([dq, dk, dv], axis=0).transpose(1, 3, 0, 2, 4).reshape(T, J)
    x = f64(img).reshape(T, HID)
    dx = mxq(dy, 1, "e5m2") @ mxq(f64(W_img_qkv), 0, "e4m3")
    dw = mxq(dy, 0, "e5m2").T @ mxq(x, 0, "e4m3")
    return dx.reshape(B, N, HID), dw

@@ -1,0 +1,605 @@
+from contextlib import ExitStack
+
+import concourse.mybir as mybir
+from concourse.masks import make_identity
+
+TOKENS, HID, HEADS, HEAD = 1024, 768, 8, 128
+FEATURES = 3 * HEADS * HEAD
+FLOPS = 2 * 2 * TOKENS * FEATURES * HID
+
+F32 = mybir.dt.float32
+BF16 = mybir.dt.bfloat16
+U32 = mybir.dt.uint32
+U8 = mybir.dt.uint8
+E4M3 = mybir.dt.float8_e4m3fn_x4
+E5M2 = mybir.dt.float8_e5m2_x4
+ADD = mybir.AluOpType.add
+SUB = mybir.AluOpType.subtract
+MUL = mybir.AluOpType.mult
+
+P = 128
+SCHEDULE = [
+    ('D', 'load', 'rope'),
+    ('D', 'load', 'v00'),
+    ('D', 'load', 'i0'),
+    ('V', 'dup', 0),
+    ('V', 'dup', 1),
+    ('P', 'tab1', 0),
+    ('D', 'load', 'v10'),
+    ('P', 'tab1', 1),
+    ('S', 'tabcopy', 0),
+    ('V', 'sortv', 'v00', 0),
+    ('S', 'tabcopy', 1),
+    ('P', 'tab2', 0),
+    ('V', 'sortv', 'v00', 1),
+    ('D', 'load', 'q00'),
+    ('P', 'tab2', 1),
+    ('V', 'quantA', 'v00'),
+    ('P', 'turn', 'v00', 0),
+    ('S', 'interleave', 'i0', 0),
+    ('D', 'load', 'i1'),
+    ('P', 'turn', 'v00', 1),
+    ('V', 'copyB', 'v00', 0),
+    ('S', 'sortv', 'v10', 0),
+    ('V', 'interleave', 'i0', 1),
+    ('D', 'load', 'v01'),
+    ('V', 'copyB', 'v00', 1),
+    ('S', 'interleave', 'i0', 2),
+    ('V', 'mult', 'q00', 0),
+    ('D', 'load', 'v11'),
+    ('S', 'sortv', 'v10', 1),
+    ('D', 'load', 'w4'),
+    ('S', 'interleave', 'i1', 0),
+    ('P', 'turn', 'v10', 0),
+    ('V', 'quantB', 'v00'),
+    ('P', 'turn', 'v10', 1),
+    ('G', 'add', 'q00', 0, 0),
+    ('S', 'copyB', 'v10', 0),
+    ('D', 'load', 'w5'),
+    ('V', 'quantK', 'i0', 0),
+    ('S', 'interleave', 'i1', 1),
+    ('G', 'add', 'q00', 0, 1),
+    ('D', 'load', 'q10'),
+    ('S', 'copyB', 'v10', 1),
+    ('V', 'quantK', 'i0', 1),
+    ('V', 'quantA', 'v10'),
+    ('S', 'interleave', 'i1', 2),
+    ('D', 'load', 'q01'),
+    ('V', 'quantB', 'v10'),
+    ('V', 'quantK', 'i1', 0),
+    ('S', 'sortv', 'v01', 0),
+    ('D', 'load', 'q11'),
+    ('V', 'quantK', 'i1', 1),
+    ('V', 'mult', 'q00', 1),
+    ('P', 'dw', 'v', '0', 0),
+    ('S', 'sortv', 'v11', 0),
+    ('D', 'load', 'w0'),
+    ('P', 'dw', 'v', '0', 1),
+    ('S', 'outc', 'w', 'v', '0', 0, 0),
+    ('V', 'mult', 'q10', 0),
+    ('G', 'add', 'q00', 1, 0),
+    ('S', 'outc', 'w', 'v', '0', 0, 1),
+    ('S', 'outc', 'w', 'v', '0', 1, 0),
+    ('P', 'dw', 'v', '0', 2),
+    ('S', 'outc', 'w', 'v', '0', 1, 1),
+    ('G', 'add', 'q00', 1, 1),
+    ('S', 'sortv', 'v01', 1),
+    ('D', 'store', 'w', 'v', '0', 0),
+    ('P', 'dw', 'v', '0', 3),
+    ('V', 'mult', 'q01', 0),
+    ('S', 'outc', 'w', 'v', '0', 2, 0),
+    ('P', 'turn', 'q00', 0),
+    ('S', 'outc', 'w', 'v', '0', 2, 1),
+    ('P', 'turn', 'v01', 0),
+    ('S', 'outc', 'w', 'v', '0', 3, 0),
+    ('S', 'outc', 'w', 'v', '0', 3, 1),
+    ('V', 'quantA', 'v01'),
+    ('S', 'copyB', 'v01', 0),
+    ('D', 'store', 'w', 'v', '0', 1),
+    ('V', 'quantA', 'q00'),
+    ('S', 'sortv', 'v11', 1),
+    ('P', 'turn', 'v01', 1),
+    ('V', 'mult', 'q10', 1),
+    ('G', 'add', 'q10', 0, 0),
+    ('S', 'copyB', 'v01', 1),
+    ('G', 'add', 'q10', 0, 1),
+    ('V', 'copyB', 'q00', 0),
+    ('S', 'interleave', 'w4', 0),
+    ('P', 'turn', 'v11', 0),
+    ('G', 'add', 'q10', 1, 0),
+    ('V', 'mult', 'q01', 1),
+    ('P', 'turn', 'v11', 1),
+    ('S', 'copyB', 'v11', 0),
+    ('G', 'add', 'q10', 1, 1),
+    ('S', 'interleave', 'w4', 1),
+    ('P', 'turn', 'q00', 1),
+    ('G', 'add', 'q01', 0, 0),
+    ('V', 'mult', 'q11', 0),
+    ('S', 'copyB', 'v11', 1),
+    ('G', 'add', 'q01', 0, 1),
+    ('S', 'copyB', 'q00', 1),
+    ('P', 'turn', 'q10', 0),
+    ('V', 'quantB', 'v01'),
+    ('S', 'interleave', 'w4', 2),
+    ('P', 'turn', 'q10', 1),
+    ('G', 'add', 'q01', 1, 0),
+    ('S', 'interleave', 'w5', 0),
+    ('D', 'load', 'w1'),
+    ('V', 'quantA', 'v11'),
+    ('G', 'add', 'q01', 1, 1),
+    ('P', 'dw', 'v', '1', 0),
+    ('S', 'copyB', 'q10', 0),
+    ('D', 'load', 'k00'),
+    ('V', 'quantB', 'v11'),
+    ('S', 'interleave', 'w5', 1),
+    ('P', 'dw', 'v', '1', 1),
+    ('G', 'add', 'q11', 0, 0),
+    ('D', 'load', 'k10'),
+    ('P', 'turn', 'q01', 0),
+    ('S', 'outc', 'w', 'v', '1', 0, 0),
+    ('V', 'quantK', 'w4', 0),
+    ('S', 'outc', 'w', 'v', '1', 0, 1),
+    ('S', 'outc', 'w', 'v', '1', 1, 0),
+    ('P', 'dw', 'v', '1', 2),
+    ('G', 'add', 'q11', 0, 1),
+    ('S', 'outc', 'w', 'v', '1', 1, 1),
+    ('S', 'interleave', 'w5', 2),
+    ('D', 'store', 'w', 'v', '1', 0),
+    ('P', 'dw', 'v', '1', 3),
+    ('V', 'quantK', 'w4', 1),
+    ('V', 'quantK', 'w5', 0),
+    ('S', 'outc', 'w', 'v', '1', 2, 0),
+    ('V', 'quantK', 'w5', 1),
+    ('V', 'quantB', 'q00'),
+    ('S', 'outc', 'w', 'v', '1', 2, 1),
+    ('D', 'load', 'w2'),
+    ('S', 'outc', 'w', 'v', '1', 3, 0),
+    ('P', 'dxA', 1, 0, 'v0,v1'),
+    ('V', 'quantA', 'q10'),
+    ('S', 'outc', 'w', 'v', '1', 3, 1),
+    ('S', 'copyB', 'q10', 1),
+    ('V', 'quantA', 'q01'),
+    ('P', 'dxA', 1, 1, 'v0,v1'),
+    ('V', 'mult', 'q11', 1),
+    ('D', 'store', 'w', 'v', '1', 1),
+    ('S', 'outA', 'x', 1, 0, 0),
+    ('P', 'turn', 'q01', 1),
+    ('S', 'outA', 'x', 1, 0, 1),
+    ('S', 'outA', 'x', 1, 1, 0),
+    ('P', 'dxA', 1, 2, 'v0,v1'),
+    ('S', 'outA', 'x', 1, 1, 1),
+    ('S', 'copyB', 'q01', 0),
+    ('V', 'mult', 'k00', 0),
+    ('G', 'add', 'q11', 1, 0),
+    ('P', 'dxA', 1, 3, 'v0,v1'),
+    ('S', 'outA', 'x', 1, 2, 0),
+    ('G', 'add', 'q11', 1, 1),
+    ('S', 'outA', 'x', 1, 2, 1),
+    ('S', 'outA', 'x', 1, 3, 0),
+    ('P', 'dw', 'q', '0', 0),
+    ('V', 'mult', 'k10', 0),
+    ('S', 'outA', 'x', 1, 3, 1),
+    ('G', 'add', 'k00', 0, 0),
+    ('S', 'copyB', 'q01', 1),
+    ('P', 'dw', 'q', '0', 1),
+    ('S', 'outc', 'w', 'q', '0', 0, 0),
+    ('G', 'add', 'k00', 0, 1),
+    ('P', 'turn', 'q11', 0),
+    ('S', 'outc', 'w', 'q', '0', 0, 1),
+    ('V', 'mult', 'k00', 1),
+    ('S', 'outc', 'w', 'q', '0', 1, 0),
+    ('P', 'dw', 'q', '0', 2),
+    ('G', 'add', 'k10', 0, 0),
+    ('S', 'outc', 'w', 'q', '0', 1, 1),
+    ('S', 'copyB', 'q11', 0),
+    ('D', 'store', 'w', 'q', '0', 0),
+    ('P', 'dw', 'q', '0', 3),
+    ('G', 'add', 'k10', 0, 1),
+    ('S', 'outc', 'w', 'q', '0', 2, 0),
+    ('V', 'mult', 'k10', 1),
+    ('S', 'outc', 'w', 'q', '0', 2, 1),
+    ('P', 'turn', 'q11', 1),
+    ('S', 'outc', 'w', 'q', '0', 3, 0),
+    ('G', 'add', 'k00', 1, 0),
+    ('S', 'outc', 'w', 'q', '0', 3, 1),
+    ('S', 'copyB', 'q11', 1),
+    ('D', 'store', 'w', 'q', '0', 1),
+    ('V', 'quantB', 'q10'),
+    ('S', 'interleave', 'w0', 0),
+    ('G', 'add', 'k00', 1, 1),
+    ('S', 'interleave', 'w1', 0),
+    ('V', 'quantB', 'q01'),
+    ('P', 'turn', 'k00', 0),
+    ('G', 'add', 'k10', 1, 0),
+    ('P', 'turn', 'k00', 1),
+    ('S', 'interleave', 'w0', 1),
+    ('V', 'quantA', 'q11'),
+    ('S', 'interleave', 'w1', 1),
+    ('G', 'add', 'k10', 1, 1),
+    ('P', 'dw', 'q', '1', 0),
+    ('V', 'quantB', 'q11'),
+    ('S', 'interleave', 'w0', 2),
+    ('P', 'dw', 'q', '1', 1),
+    ('V', 'quantK', 'w0', 0),
+    ('V', 'quantK', 'w1', 0),
+    ('S', 'outc', 'w', 'q', '1', 0, 0),
+    ('D', 'load', 'w3'),
+    ('V', 'quantK', 'w0', 1),
+    ('S', 'outc', 'w', 'q', '1', 0, 1),
+    ('V', 'quantA', 'k00'),
+    ('S', 'outc', 'w', 'q', '1', 1, 0),
+    ('P', 'dw', 'q', '1', 2),
+    ('V', 'quantA', 'k10'),
+    ('S', 'outc', 'w', 'q', '1', 1, 1),
+    ('S', 'interleave', 'w1', 2),
+    ('V', 'copyB', 'k00', 0),
+    ('P', 'dw', 'q', '1', 3),
+    ('D', 'load', 'k01'),
+    ('S', 'outc', 'w', 'q', '1', 2, 0),
+    ('V', 'quantK', 'w1', 1),
+    ('P', 'turn', 'k10', 0),
+    ('D', 'load', 'k11'),
+    ('V', 'outc', 'w', 'q', '1', 2, 1),
+    ('S', 'outc', 'w', 'q', '1', 3, 0),
+    ('V', 'outc', 'w', 'q', '1', 3, 1),
+    ('P', 'dxA', 0, 0, 'v0,v1,q0,q1'),
+    ('V', 'copyB', 'k00', 1),
+    ('S', 'copyB', 'k10', 0),
+    ('D', 'store', 'w', 'q', '1', 0),
+    ('V', 'interleave', 'w2', 0),
+    ('S', 'interleave', 'w3', 0),
+    ('V', 'quantB', 'k00'),
+    ('P', 'dxA', 0, 1, 'v0,v1,q0,q1'),
+    ('V', 'mult', 'k01', 0),
+    ('D', 'store', 'w', 'q', '1', 1),
+    ('S', 'outA', 'x', 0, 0, 0),
+    ('S', 'outA', 'x', 0, 0, 1),
+    ('S', 'interleave', 'w2', 1),
+    ('P', 'dxA', 0, 2, 'v0,v1,q0,q1'),
+    ('V', 'mult', 'k11', 0),
+    ('S', 'outA', 'x', 0, 1, 0),
+    ('G', 'add', 'k01', 0, 0),
+    ('S', 'outA', 'x', 0, 1, 1),
+    ('S', 'interleave', 'w2', 2),
+    ('G', 'add', 'k01', 0, 1),
+    ('P', 'dxA', 0, 3, 'v0,v1,q0,q1'),
+    ('S', 'outA', 'x', 0, 2, 0),
+    ('V', 'mult', 'k01', 1),
+    ('G', 'add', 'k11', 0, 0),
+    ('S', 'outA', 'x', 0, 2, 1),
+    ('S', 'interleave', 'w3', 1),
+    ('G', 'add', 'k11', 0, 1),
+    ('P', 'turn', 'k10', 1),
+    ('S', 'outA', 'x', 0, 3, 0),
+    ('V', 'mult', 'k11', 1),
+    ('S', 'outA', 'x', 0, 3, 1),
+    ('P', 'dw', 'k', '0', 0),
+    ('S', 'copyB', 'k10', 1),
+    ('G', 'add', 'k01', 1, 0),
+    ('P', 'dw', 'k', '0', 1),
+    ('S', 'outc', 'w', 'k', '0', 0, 0),
+    ('G', 'add', 'k01', 1, 1),
+    ('S', 'outc', 'w', 'k', '0', 0, 1),
+    ('P', 'dw', 'k', '0', 2),
+    ('S', 'outc', 'w', 'k', '0', 1, 0),
+    ('V', 'quantK', 'w2', 0),
+    ('S', 'outc', 'w', 'k', '0', 1, 1),
+    ('S', 'interleave', 'w3', 2),
+    ('G', 'add', 'k11', 1, 0),
+    ('P', 'turn', 'k01', 0),
+    ('D', 'store', 'w', 'k', '0', 0),
+    ('P', 'turn', 'k01', 1),
+    ('V', 'quantK', 'w2', 1),
+    ('P', 'dw', 'k', '0', 3),
+    ('S', 'outc', 'w', 'k', '0', 2, 0),
+    ('G', 'add', 'k11', 1, 1),
+    ('S', 'outc', 'w', 'k', '0', 2, 1),
+    ('S', 'copyB', 'k01', 0),
+    ('P', 'dxB', 0, 0, 'k0'),
+    ('V', 'quantK', 'w3', 0),
+    ('S', 'outc', 'w', 'k', '0', 3, 0),
+    ('P', 'turn', 'k11', 0),
+    ('V', 'quantK', 'w3', 1),
+    ('V', 'quantB', 'k10'),
+    ('S', 'outc', 'w', 'k', '0', 3, 1),
+    ('S', 'copyB', 'k01', 1),
+    ('P', 'dxB', 0, 1, 'k0'),
+    ('V', 'quantA', 'k01'),
+    ('D', 'store', 'w', 'k', '0', 1),
+    ('V', 'quantA', 'k11'),
+    ('S', 'copyB', 'k11', 0),
+    ('P', 'turn', 'k11', 1),
+    ('V', 'quantB', 'k01'),
+    ('P', 'dxB', 0, 0, 'k1'),
+    ('S', 'copyB', 'k11', 1),
+    ('P', 'dxB', 0, 1, 'k1'),
+    ('V', 'outc', 'x', 0, 0, 0),
+    ('V', 'outc', 'x', 0, 0, 1),
+    ('V', 'outc', 'x', 0, 1, 0),
+    ('P', 'dxB', 0, 2, 'k0'),
+    ('P', 'dxB', 0, 2, 'k1'),
+    ('V', 'outc', 'x', 0, 1, 1),
+    ('V', 'quantB', 'k11'),
+    ('D', 'store', 'x', 0, 0),
+    ('P', 'dxB', 0, 3, 'k0'),
+    ('V', 'outc', 'x', 0, 2, 0),
+    ('P', 'dxB', 0, 3, 'k1'),
+    ('V', 'outc', 'x', 0, 2, 1),
+    ('P', 'dw', 'k', '1', 0),
+    ('V', 'outc', 'x', 0, 3, 0),
+    ('V', 'outc', 'x', 0, 3, 1),
+    ('P', 'dw', 'k', '1', 1),
+    ('V', 'outc', 'w', 'k', '1', 0, 1),
+    ('S', 'outc', 'w', 'k', '1', 0, 0),
+    ('D', 'store', 'x', 0, 1),
+    ('P', 'dw', 'k', '1', 2),
+    ('V', 'outc', 'w', 'k', '1', 1, 1),
+    ('S', 'outc', 'w', 'k', '1', 1, 0),
+    ('D', 'store', 'w', 'k', '1', 0),
+    ('P', 'dw', 'k', '1', 3),
+    ('V', 'outc', 'w', 'k', '1', 2, 1),
+    ('S', 'outc', 'w', 'k', '1', 2, 0),
+    ('P', 'dxB', 1, 0, 'q0,q1,k0'),
+    ('V', 'outc', 'w', 'k', '1', 3, 1),
+    ('S', 'outc', 'w', 'k', '1', 3, 0),
+    ('D', 'store', 'w', 'k', '1', 1),
+    ('P', 'dxB', 1, 0, 'k1'),
+    ('P', 'dxB', 1, 1, 'q0,q1,k0'),
+    ('V', 'outc', 'x', 1, 0, 0),
+    ('V', 'outc', 'x', 1, 0, 1),
+    ('P', 'dxB', 1, 1, 'k1'),
+    ('P', 'dxB', 1, 2, 'q0,q1,k0'),
+    ('V', 'outc', 'x', 1, 1, 0),
+    ('V', 'outc', 'x', 1, 1, 1),
+    ('D', 'store', 'x', 1, 0),
+    ('P', 'dxB', 1, 2, 'k1'),
+    ('P', 'dxB', 1, 3, 'q0,q1,k0'),
+    ('V', 'outc', 'x', 1, 2, 0),
+    ('V', 'outc', 'x', 1, 2, 1),
+    ('P', 'dxB', 1, 3, 'k1'),
+    ('V', 'outc', 'x', 1, 3, 0),
+    ('V', 'outc', 'x', 1, 3, 1),
+    ('D', 'store', 'x', 1, 1),
+]
+
+
+def tile_jointattention_pa_v_kernel(tc, img, rope, W_img_qkv, grad_0, grad_1, grad_2, out_0, out_1):
+    nc = tc.nc
+    names = "qkv"
+    grads = {n: a.rearrange("b (s h) (g p j) d -> b s g p h (j d)", s=2, g=2, p=P, j=4) for n, a in zip(names, (grad_0, grad_1, grad_2))}
+    img_v = img.rearrange("b (g p j) c -> b g p j c", g=2, p=P, j=4)
+    w_v = W_img_qkv.rearrange("(s p j) c -> s p j c", s=6, p=P, j=4)
+    rope_v = rope.rearrange("b (g p j) d -> b p g (j d)", g=2, p=P, j=4)
+    out0_v = out_0.rearrange("b (g p j) c -> b g p j c", g=2, p=P, j=4)
+    out1_v = out_1.rearrange("(s m t) c -> s m t c", s=6, m=P, t=4)
+
+    with ExitStack() as ctx:
+        const = ctx.enter_context(tc.tile_pool(name="const", bufs=1))
+        gpool = ctx.enter_context(tc.tile_pool(name="gpool", bufs=7))
+        raw = ctx.enter_context(tc.tile_pool(name="raw", bufs=3))
+        inter = ctx.enter_context(tc.tile_pool(name="inter", bufs=3))
+        prod = ctx.enter_context(tc.tile_pool(name="prod", bufs=3))
+        dyp = ctx.enter_context(tc.tile_pool(name="dyp", bufs=3))
+        apool = ctx.enter_context(tc.tile_pool(name="apool", bufs=8))
+        bpool = ctx.enter_context(tc.tile_pool(name="bpool", bufs=10))
+        outp = ctx.enter_context(tc.tile_pool(name="outp", bufs=8))
+        tabp = ctx.enter_context(tc.psum_pool(name="tabp", bufs=1))
+        tpp = ctx.enter_context(tc.psum_pool(name="tpp", bufs=2))
+        accp = ctx.enter_context(tc.psum_pool(name="accp", bufs=4))
+        ctx.enter_context(tc.manual_schedule())
+
+        ident = const.tile([P, P], F32)
+        ident_bf = const.tile([P, P], BF16)
+        rope_sb = const.tile([P, 2, 512], BF16)
+        w_codes = const.tile([P, 6, HID], U32, align_bytes=64)
+        w_scales = const.tile([P, 6, HID], U8, align_bytes=64)
+        i_codes = const.tile([P, 2, HID], U32, align_bytes=64)
+        i_scales = const.tile([P, 2, HID], U8, align_bytes=64)
+        live = {}
+        make_identity(nc, ident_bf[:])
+        make_identity(nc, ident[:])
+
+        def copy(engine, out, in_):
+            if engine == "V":
+                nc.vector.tensor_copy(out=out, in_=in_)
+            elif engine == "S":
+                nc.scalar.copy(out=out, in_=in_)
+
+        def load(engine, u):
+            if u == "rope":
+                nc.sync.dma_start(out=rope_sb[:], in_=rope_v[0])
+            elif u[0] == "i":
+                rtile = raw.tile([P, 4, HID], BF16, align_bytes=64)
+                nc.sync.dma_start(out=rtile[:], in_=img_v[0, int(u[1])])
+                live["raw", u] = rtile
+            elif u[0] == "w":
+                rtile = raw.tile([P, 4, HID], BF16, align_bytes=64)
+                nc.sync.dma_start(out=rtile[:], in_=w_v[int(u[1])])
+                live["raw", u] = rtile
+            else:
+                gtile = gpool.tile([P, 4, 512], BF16, align_bytes=64)
+                nc.sync.dma_start(out=gtile[:], in_=grads[u[0]][0, int(u[2]), int(u[1])])
+                live["g", u] = gtile
+
+        def interleave(engine, u, pc):
+            if pc != 1:
+                it = inter.tile([P, 512, 4], BF16, align_bytes=64)
+                live["it", u, pc // 2] = it
+            lo = 256 * (pc % 2)
+            copy(engine, live["it", u, pc // 2][:, lo:lo + 256, :], live["raw", u][:, :, 256 * pc:256 * pc + 256].rearrange("p j w -> p w j"))
+
+        def quantK(engine, u, part):
+            n = 512 - 256 * part
+            lo = 512 * part
+            codes, scales = (i_codes, i_scales) if u[0] == "i" else (w_codes, w_scales)
+            nc.vector.quantize_mx(
+                out=codes[:, int(u[1]), lo:lo + n].bitcast(E4M3),
+                scales=scales[:, int(u[1]), lo:lo + n],
+                in_=live["it", u, part][:, 0:n, :].rearrange("p w j -> p (w j)"),
+            )
+
+        def dup(engine, which):
+            pairs = rope_sb[:].rearrange("p g (n e) -> p (g n) e", e=2)
+            d = dyp.tile([P, 512, 2], BF16, tag="dya", align_bytes=64)
+            copy(engine, d[:], pairs[:, :, which:which + 1].to_broadcast([P, 512, 2]))
+            live["dup", which] = d
+
+        def tab1(engine, which):
+            flat = live["dup", which][:].rearrange("p n e -> p (n e)")
+            turned = tpp.tile([P, 8, P], BF16, tag="tp")
+            for b in range(8):
+                nc.tensor.transpose(turned[:, b, :], flat[:, b * P:(b + 1) * P], ident_bf[:])
+            live["turned", which] = turned
+
+        def tabcopy(engine, which):
+            back = dyp.tile([P, 8, P], BF16, tag="dyb", align_bytes=64)
+            copy(engine, back[:], live["turned", which][:])
+            live["back", which] = back
+
+        def tab2(engine, which):
+            table = tabp.tile([P, 8, P], BF16, name="table%d" % which)
+            for b in range(8):
+                nc.tensor.transpose(table[:, b, :], live["back", which][:, b, :], ident_bf[:])
+            live["table", which] = table
+
+        def sortv(engine, u, part):
+            if part == 0:
+                d = dyp.tile([P, 4, P, 4], BF16, tag="dya", align_bytes=64)
+                live["dya", u] = d
+            d = live["dya", u]
+            for h in range(2 * part, 2 * part + 2):
+                copy(
+                    engine,
+                    d[:, :, h * 32:(h + 1) * 32, :].rearrange("p t q j -> p q t j"),
+                    live["g", u][:, h, :].rearrange("p (j q t) -> p q t j", j=4, t=4),
+                )
+
+        def mult(engine, u, part):
+            g = int(u[1])
+            for which in range(2):
+                pt = prod.tile([P, 4, 64, 4], F32, name="prod%d" % which, align_bytes=64)
+                live["prod", u, part, which] = pt
+            for hh in range(2):
+                for which in range(2):
+                    nc.vector.tensor_tensor(
+                        out=live["prod", u, part, which][:, :, hh * 32:(hh + 1) * 32, :].rearrange("p t q j -> p q t j"),
+                        in0=live["g", u][:, 2 * part + hh, :].rearrange("p (j q t) -> p q t j", j=4, t=4),
+                        in1=live["table", which][:, 4 * g:4 * g + 4, :].rearrange("p j (q t) -> p q t j", t=4),
+                        op=MUL,
+                    )
+
+        def add(engine, u, part, e):
+            if part == 0 and e == 0:
+                d = dyp.tile([P, 4, P, 4], BF16, tag="dya", align_bytes=64)
+                live["dya", u] = d
+            d = live["dya", u][:].rearrange("p (a e) q j -> p a e (q j)", e=2)
+            p0 = live["prod", u, part, 0][:].rearrange("p (a e) q j -> p a e (q j)", e=2)
+            p1 = live["prod", u, part, 1][:].rearrange("p (a e) q j -> p a e (q j)", e=2)
+            eng = nc.gpsimd if engine == "G" else nc.vector
+            eng.tensor_tensor(
+                out=d[:, :, e, part * 256:(part + 1) * 256], in0=p0[:, :, e, :], in1=p1[:, :, 1 - e, :], op=ADD if e == 0 else SUB
+            )
+
+        def quantA(engine, u):
+            ac = apool.tile([P, 512], U32, align_bytes=64)
+            asc = apool.tile([P, 512], U8, align_bytes=64)
+            nc.vector.quantize_mx(out=ac[:].bitcast(E5M2), scales=asc[:], in_=live["dya", u][:].rearrange("p t q j -> p (t q j)"))
+            live["A", u] = (ac, asc)
+
+        def turn(engine, u, pair):
+            words = live["dya", u][:].rearrange("p t q j -> p (t q j)").bitcast(F32)
+            tp = tpp.tile([P, 4, P], F32, tag="tp")
+            for t in range(4):
+                nc.tensor.transpose(tp[:, t, :], words[:, t * 256 + pair:(t + 1) * 256:2], ident[:])
+            live["tp", u, pair] = tp
+
+        def copyB(engine, u, pair):
+            if pair == 0:
+                db = dyp.tile([P, 2, 1024], BF16, tag="dyb", align_bytes=64)
+                live["dyb", u] = db
+            copy(
+                engine,
+                live["dyb", u][:, pair, :].rearrange("p (e c t) -> p e c t", e=2, t=4),
+                live["tp", u, pair][:].rearrange("p t c -> p (t c)").bitcast(BF16).rearrange("p (t c e) -> p e c t", t=4, e=2),
+            )
+
+        def quantB(engine, u):
+            bc = bpool.tile([P, 512], U32, align_bytes=64)
+            bsc = bpool.tile([P, 512], U8, align_bytes=64)
+            nc.vector.quantize_mx(out=bc[:].bitcast(E5M2), scales=bsc[:], in_=live["dyb", u][:].rearrange("p u c -> p (u c)"))
+            live["B", u] = (bc, bsc)
+
+        def mm(key, half, lhs, cols, rhs, n, start, stop):
+            codes, scales = lhs
+            rc, rs = rhs
+            c = slice(256 * half, 256 * half + 512)
+            nc.tensor.matmul_mx(
+                out=live["acc", key, half][:], lhsT=codes[:, cols].bitcast(E5M2), lhsT_scale=scales[:, cols],
+                rhs=rc[:, n, c].bitcast(E4M3), rhs_scale=rs[:, n, c], start=start, stop=stop,
+            )
+
+        def open_acc(key):
+            for half in range(2):
+                acc = accp.tile([P, 512], F32)
+                live["acc", key, half] = acc
+
+        def dw(engine, x, s, t):
+            key = ("w", x, s, t)
+            open_acc(key)
+            for g in range(2):
+                for half in range(2):
+                    mm(key, half, live["A", "%s%d%s" % (x, g, s)], slice(t * P, (t + 1) * P), (i_codes, i_scales), g, g == 0, g == 1)
+
+        STAGE = {('A', 0): ['v0', 'v1', 'q0', 'q1'], ('A', 1): ['v0', 'v1'], ('B', 0): ['k0', 'k1'], ('B', 1): ['q0', 'q1', 'k0', 'k1']}
+
+        def dx(stage, g, j, units):
+            key = ("x" + stage, g, j)
+            members = STAGE[stage, g]
+            for u in units.split(","):
+                if u == members[0]:
+                    open_acc(key)
+                for half in range(2):
+                    mm(key, half, live["B", "%s%s%s" % (u[0], g, u[1])], slice(j * P, (j + 1) * P), (w_codes, w_scales),
+                       2 * names.index(u[0]) + int(u[1]), u == members[0], u == members[-1])
+
+        def result(group):
+            if ("res", group) not in live:
+                res = outp.tile([P, 2, HID], F32)
+                live["res", group] = res
+            return live["res", group]
+
+        def halves(key, pos, group, half):
+            a = live["acc", key, half]
+            res = result(group)
+            if half == 0:
+                return res[:, pos % 2, 0:512], a[:]
+            return res[:, pos % 2, 512:768], a[:, 256:512]
+
+        def outA(engine, x, g, j, half):
+            out, in_ = halves(("xA", g, j), j, ("x", g, j // 2), half)
+            copy(engine, out, in_)
+
+        def outc(engine, *key):
+            half = key[-1]
+            pos = key[-2]
+            group = key[:-2] + (pos // 2,)
+            if key[0] == "w":
+                out, in_ = halves(key[:-1], pos, group, half)
+                copy(engine, out, in_)
+            else:
+                out, in_ = halves(("xB",) + key[1:-1], pos, group, half)
+                nc.vector.tensor_tensor(out=out, in0=in_, in1=out, op=ADD)
+
+        def store(engine, *key):
+            th = key[-1]
+            if key[0] == "w":
+                dst = out1_v[2 * names.index(key[1]) + int(key[2]), :, 2 * th:2 * th + 2, :]
+            else:
+                dst = out0_v[0, key[1], :, 2 * th:2 * th + 2, :]
+            nc.sync.dma_start(out=dst, in_=live["res", key][:])
+
+        RUN = {"load": load, "interleave": interleave, "quantK": quantK, "dup": dup, "tab1": tab1, "tabcopy": tabcopy, "tab2": tab2, "sortv": sortv,
+               "mult": mult, "add": add, "quantA": quantA, "turn": turn, "copyB": copyB, "quantB": quantB, "dw": dw,
+               "dxA": lambda e, *a: dx("A", *a), "dxB": lambda e, *a: dx("B", *a), "outA": outA, "outc": outc, "store": store}
+        for step in SCHEDULE:
+            RUN[step[1]](step[0], *step[2:])

@@ -3,8 +3,7 @@ from contextlib import ExitStack
 import concourse.mybir as mybir
 from concourse.masks import make_identity
 
-TOKENS, HID, HEADS, HEAD = 1024, 768, 8, 128
-FEATURES = 3 * HEADS * HEAD
+TOKENS, HID, FEATURES = 1024, 768, 3072
 FLOPS = 2 * 2 * TOKENS * FEATURES * HID
 
 F32 = mybir.dt.float32
@@ -13,593 +12,318 @@ U32 = mybir.dt.uint32
 U8 = mybir.dt.uint8
 E4M3 = mybir.dt.float8_e4m3fn_x4
 E5M2 = mybir.dt.float8_e5m2_x4
-ADD = mybir.AluOpType.add
-SUB = mybir.AluOpType.subtract
-MUL = mybir.AluOpType.mult
 
 P = 128
-SCHEDULE = [
-    ('D', 'load', 'rope'),
-    ('D', 'load', 'v00'),
-    ('D', 'load', 'i0'),
-    ('V', 'dup', 0),
-    ('V', 'dup', 1),
-    ('P', 'tab1', 0),
-    ('D', 'load', 'v10'),
-    ('P', 'tab1', 1),
-    ('S', 'tabcopy', 0),
-    ('V', 'sortv', 'v00', 0),
-    ('S', 'tabcopy', 1),
-    ('P', 'tab2', 0),
-    ('V', 'sortv', 'v00', 1),
-    ('D', 'load', 'q00'),
-    ('P', 'tab2', 1),
-    ('V', 'quantA', 'v00'),
-    ('P', 'turn', 'v00', 0),
-    ('S', 'interleave', 'i0', 0),
-    ('D', 'load', 'i1'),
-    ('P', 'turn', 'v00', 1),
-    ('V', 'copyB', 'v00', 0),
-    ('S', 'sortv', 'v10', 0),
-    ('V', 'interleave', 'i0', 1),
-    ('D', 'load', 'v01'),
-    ('V', 'copyB', 'v00', 1),
-    ('S', 'interleave', 'i0', 2),
-    ('V', 'mult', 'q00', 0),
-    ('D', 'load', 'v11'),
-    ('S', 'sortv', 'v10', 1),
-    ('D', 'load', 'w4'),
-    ('S', 'interleave', 'i1', 0),
-    ('P', 'turn', 'v10', 0),
-    ('V', 'quantB', 'v00'),
-    ('P', 'turn', 'v10', 1),
-    ('G', 'add', 'q00', 0, 0),
-    ('S', 'copyB', 'v10', 0),
-    ('D', 'load', 'w5'),
-    ('V', 'quantK', 'i0', 0),
-    ('S', 'interleave', 'i1', 1),
-    ('G', 'add', 'q00', 0, 1),
-    ('D', 'load', 'q10'),
-    ('S', 'copyB', 'v10', 1),
-    ('V', 'quantK', 'i0', 1),
-    ('V', 'quantA', 'v10'),
-    ('S', 'interleave', 'i1', 2),
-    ('D', 'load', 'q01'),
-    ('V', 'quantB', 'v10'),
-    ('V', 'quantK', 'i1', 0),
-    ('S', 'sortv', 'v01', 0),
-    ('D', 'load', 'q11'),
-    ('V', 'quantK', 'i1', 1),
-    ('V', 'mult', 'q00', 1),
-    ('P', 'dw', 'v', '0', 0),
-    ('S', 'sortv', 'v11', 0),
-    ('D', 'load', 'w0'),
-    ('P', 'dw', 'v', '0', 1),
-    ('S', 'outc', 'w', 'v', '0', 0, 0),
-    ('V', 'mult', 'q10', 0),
-    ('G', 'add', 'q00', 1, 0),
-    ('S', 'outc', 'w', 'v', '0', 0, 1),
-    ('S', 'outc', 'w', 'v', '0', 1, 0),
-    ('P', 'dw', 'v', '0', 2),
-    ('S', 'outc', 'w', 'v', '0', 1, 1),
-    ('G', 'add', 'q00', 1, 1),
-    ('S', 'sortv', 'v01', 1),
-    ('D', 'store', 'w', 'v', '0', 0),
-    ('P', 'dw', 'v', '0', 3),
-    ('V', 'mult', 'q01', 0),
-    ('S', 'outc', 'w', 'v', '0', 2, 0),
-    ('P', 'turn', 'q00', 0),
-    ('S', 'outc', 'w', 'v', '0', 2, 1),
-    ('P', 'turn', 'v01', 0),
-    ('S', 'outc', 'w', 'v', '0', 3, 0),
-    ('S', 'outc', 'w', 'v', '0', 3, 1),
-    ('V', 'quantA', 'v01'),
-    ('S', 'copyB', 'v01', 0),
-    ('D', 'store', 'w', 'v', '0', 1),
-    ('V', 'quantA', 'q00'),
-    ('S', 'sortv', 'v11', 1),
-    ('P', 'turn', 'v01', 1),
-    ('V', 'mult', 'q10', 1),
-    ('G', 'add', 'q10', 0, 0),
-    ('S', 'copyB', 'v01', 1),
-    ('G', 'add', 'q10', 0, 1),
-    ('V', 'copyB', 'q00', 0),
-    ('S', 'interleave', 'w4', 0),
-    ('P', 'turn', 'v11', 0),
-    ('G', 'add', 'q10', 1, 0),
-    ('V', 'mult', 'q01', 1),
-    ('P', 'turn', 'v11', 1),
-    ('S', 'copyB', 'v11', 0),
-    ('G', 'add', 'q10', 1, 1),
-    ('S', 'interleave', 'w4', 1),
-    ('P', 'turn', 'q00', 1),
-    ('G', 'add', 'q01', 0, 0),
-    ('V', 'mult', 'q11', 0),
-    ('S', 'copyB', 'v11', 1),
-    ('G', 'add', 'q01', 0, 1),
-    ('S', 'copyB', 'q00', 1),
-    ('P', 'turn', 'q10', 0),
-    ('V', 'quantB', 'v01'),
-    ('S', 'interleave', 'w4', 2),
-    ('P', 'turn', 'q10', 1),
-    ('G', 'add', 'q01', 1, 0),
-    ('S', 'interleave', 'w5', 0),
-    ('D', 'load', 'w1'),
-    ('V', 'quantA', 'v11'),
-    ('G', 'add', 'q01', 1, 1),
-    ('P', 'dw', 'v', '1', 0),
-    ('S', 'copyB', 'q10', 0),
-    ('D', 'load', 'k00'),
-    ('V', 'quantB', 'v11'),
-    ('S', 'interleave', 'w5', 1),
-    ('P', 'dw', 'v', '1', 1),
-    ('G', 'add', 'q11', 0, 0),
-    ('D', 'load', 'k10'),
-    ('P', 'turn', 'q01', 0),
-    ('S', 'outc', 'w', 'v', '1', 0, 0),
-    ('V', 'quantK', 'w4', 0),
-    ('S', 'outc', 'w', 'v', '1', 0, 1),
-    ('S', 'outc', 'w', 'v', '1', 1, 0),
-    ('P', 'dw', 'v', '1', 2),
-    ('G', 'add', 'q11', 0, 1),
-    ('S', 'outc', 'w', 'v', '1', 1, 1),
-    ('S', 'interleave', 'w5', 2),
-    ('D', 'store', 'w', 'v', '1', 0),
-    ('P', 'dw', 'v', '1', 3),
-    ('V', 'quantK', 'w4', 1),
-    ('V', 'quantK', 'w5', 0),
-    ('S', 'outc', 'w', 'v', '1', 2, 0),
-    ('V', 'quantK', 'w5', 1),
-    ('V', 'quantB', 'q00'),
-    ('S', 'outc', 'w', 'v', '1', 2, 1),
-    ('D', 'load', 'w2'),
-    ('S', 'outc', 'w', 'v', '1', 3, 0),
-    ('P', 'dxA', 1, 0, 'v0,v1'),
-    ('V', 'quantA', 'q10'),
-    ('S', 'outc', 'w', 'v', '1', 3, 1),
-    ('S', 'copyB', 'q10', 1),
-    ('V', 'quantA', 'q01'),
-    ('P', 'dxA', 1, 1, 'v0,v1'),
-    ('V', 'mult', 'q11', 1),
-    ('D', 'store', 'w', 'v', '1', 1),
-    ('S', 'outA', 'x', 1, 0, 0),
-    ('P', 'turn', 'q01', 1),
-    ('S', 'outA', 'x', 1, 0, 1),
-    ('S', 'outA', 'x', 1, 1, 0),
-    ('P', 'dxA', 1, 2, 'v0,v1'),
-    ('S', 'outA', 'x', 1, 1, 1),
-    ('S', 'copyB', 'q01', 0),
-    ('V', 'mult', 'k00', 0),
-    ('G', 'add', 'q11', 1, 0),
-    ('P', 'dxA', 1, 3, 'v0,v1'),
-    ('S', 'outA', 'x', 1, 2, 0),
-    ('G', 'add', 'q11', 1, 1),
-    ('S', 'outA', 'x', 1, 2, 1),
-    ('S', 'outA', 'x', 1, 3, 0),
-    ('P', 'dw', 'q', '0', 0),
-    ('V', 'mult', 'k10', 0),
-    ('S', 'outA', 'x', 1, 3, 1),
-    ('G', 'add', 'k00', 0, 0),
-    ('S', 'copyB', 'q01', 1),
-    ('P', 'dw', 'q', '0', 1),
-    ('S', 'outc', 'w', 'q', '0', 0, 0),
-    ('G', 'add', 'k00', 0, 1),
-    ('P', 'turn', 'q11', 0),
-    ('S', 'outc', 'w', 'q', '0', 0, 1),
-    ('V', 'mult', 'k00', 1),
-    ('S', 'outc', 'w', 'q', '0', 1, 0),
-    ('P', 'dw', 'q', '0', 2),
-    ('G', 'add', 'k10', 0, 0),
-    ('S', 'outc', 'w', 'q', '0', 1, 1),
-    ('S', 'copyB', 'q11', 0),
-    ('D', 'store', 'w', 'q', '0', 0),
-    ('P', 'dw', 'q', '0', 3),
-    ('G', 'add', 'k10', 0, 1),
-    ('S', 'outc', 'w', 'q', '0', 2, 0),
-    ('V', 'mult', 'k10', 1),
-    ('S', 'outc', 'w', 'q', '0', 2, 1),
-    ('P', 'turn', 'q11', 1),
-    ('S', 'outc', 'w', 'q', '0', 3, 0),
-    ('G', 'add', 'k00', 1, 0),
-    ('S', 'outc', 'w', 'q', '0', 3, 1),
-    ('S', 'copyB', 'q11', 1),
-    ('D', 'store', 'w', 'q', '0', 1),
-    ('V', 'quantB', 'q10'),
-    ('S', 'interleave', 'w0', 0),
-    ('G', 'add', 'k00', 1, 1),
-    ('S', 'interleave', 'w1', 0),
-    ('V', 'quantB', 'q01'),
-    ('P', 'turn', 'k00', 0),
-    ('G', 'add', 'k10', 1, 0),
-    ('P', 'turn', 'k00', 1),
-    ('S', 'interleave', 'w0', 1),
-    ('V', 'quantA', 'q11'),
-    ('S', 'interleave', 'w1', 1),
-    ('G', 'add', 'k10', 1, 1),
-    ('P', 'dw', 'q', '1', 0),
-    ('V', 'quantB', 'q11'),
-    ('S', 'interleave', 'w0', 2),
-    ('P', 'dw', 'q', '1', 1),
-    ('V', 'quantK', 'w0', 0),
-    ('V', 'quantK', 'w1', 0),
-    ('S', 'outc', 'w', 'q', '1', 0, 0),
-    ('D', 'load', 'w3'),
-    ('V', 'quantK', 'w0', 1),
-    ('S', 'outc', 'w', 'q', '1', 0, 1),
-    ('V', 'quantA', 'k00'),
-    ('S', 'outc', 'w', 'q', '1', 1, 0),
-    ('P', 'dw', 'q', '1', 2),
-    ('V', 'quantA', 'k10'),
-    ('S', 'outc', 'w', 'q', '1', 1, 1),
-    ('S', 'interleave', 'w1', 2),
-    ('V', 'copyB', 'k00', 0),
-    ('P', 'dw', 'q', '1', 3),
-    ('D', 'load', 'k01'),
-    ('S', 'outc', 'w', 'q', '1', 2, 0),
-    ('V', 'quantK', 'w1', 1),
-    ('P', 'turn', 'k10', 0),
-    ('D', 'load', 'k11'),
-    ('V', 'outc', 'w', 'q', '1', 2, 1),
-    ('S', 'outc', 'w', 'q', '1', 3, 0),
-    ('V', 'outc', 'w', 'q', '1', 3, 1),
-    ('P', 'dxA', 0, 0, 'v0,v1,q0,q1'),
-    ('V', 'copyB', 'k00', 1),
-    ('S', 'copyB', 'k10', 0),
-    ('D', 'store', 'w', 'q', '1', 0),
-    ('V', 'interleave', 'w2', 0),
-    ('S', 'interleave', 'w3', 0),
-    ('V', 'quantB', 'k00'),
-    ('P', 'dxA', 0, 1, 'v0,v1,q0,q1'),
-    ('V', 'mult', 'k01', 0),
-    ('D', 'store', 'w', 'q', '1', 1),
-    ('S', 'outA', 'x', 0, 0, 0),
-    ('S', 'outA', 'x', 0, 0, 1),
-    ('S', 'interleave', 'w2', 1),
-    ('P', 'dxA', 0, 2, 'v0,v1,q0,q1'),
-    ('V', 'mult', 'k11', 0),
-    ('S', 'outA', 'x', 0, 1, 0),
-    ('G', 'add', 'k01', 0, 0),
-    ('S', 'outA', 'x', 0, 1, 1),
-    ('S', 'interleave', 'w2', 2),
-    ('G', 'add', 'k01', 0, 1),
-    ('P', 'dxA', 0, 3, 'v0,v1,q0,q1'),
-    ('S', 'outA', 'x', 0, 2, 0),
-    ('V', 'mult', 'k01', 1),
-    ('G', 'add', 'k11', 0, 0),
-    ('S', 'outA', 'x', 0, 2, 1),
-    ('S', 'interleave', 'w3', 1),
-    ('G', 'add', 'k11', 0, 1),
-    ('P', 'turn', 'k10', 1),
-    ('S', 'outA', 'x', 0, 3, 0),
-    ('V', 'mult', 'k11', 1),
-    ('S', 'outA', 'x', 0, 3, 1),
-    ('P', 'dw', 'k', '0', 0),
-    ('S', 'copyB', 'k10', 1),
-    ('G', 'add', 'k01', 1, 0),
-    ('P', 'dw', 'k', '0', 1),
-    ('S', 'outc', 'w', 'k', '0', 0, 0),
-    ('G', 'add', 'k01', 1, 1),
-    ('S', 'outc', 'w', 'k', '0', 0, 1),
-    ('P', 'dw', 'k', '0', 2),
-    ('S', 'outc', 'w', 'k', '0', 1, 0),
-    ('V', 'quantK', 'w2', 0),
-    ('S', 'outc', 'w', 'k', '0', 1, 1),
-    ('S', 'interleave', 'w3', 2),
-    ('G', 'add', 'k11', 1, 0),
-    ('P', 'turn', 'k01', 0),
-    ('D', 'store', 'w', 'k', '0', 0),
-    ('P', 'turn', 'k01', 1),
-    ('V', 'quantK', 'w2', 1),
-    ('P', 'dw', 'k', '0', 3),
-    ('S', 'outc', 'w', 'k', '0', 2, 0),
-    ('G', 'add', 'k11', 1, 1),
-    ('S', 'outc', 'w', 'k', '0', 2, 1),
-    ('S', 'copyB', 'k01', 0),
-    ('P', 'dxB', 0, 0, 'k0'),
-    ('V', 'quantK', 'w3', 0),
-    ('S', 'outc', 'w', 'k', '0', 3, 0),
-    ('P', 'turn', 'k11', 0),
-    ('V', 'quantK', 'w3', 1),
-    ('V', 'quantB', 'k10'),
-    ('S', 'outc', 'w', 'k', '0', 3, 1),
-    ('S', 'copyB', 'k01', 1),
-    ('P', 'dxB', 0, 1, 'k0'),
-    ('V', 'quantA', 'k01'),
-    ('D', 'store', 'w', 'k', '0', 1),
-    ('V', 'quantA', 'k11'),
-    ('S', 'copyB', 'k11', 0),
-    ('P', 'turn', 'k11', 1),
-    ('V', 'quantB', 'k01'),
-    ('P', 'dxB', 0, 0, 'k1'),
-    ('S', 'copyB', 'k11', 1),
-    ('P', 'dxB', 0, 1, 'k1'),
-    ('V', 'outc', 'x', 0, 0, 0),
-    ('V', 'outc', 'x', 0, 0, 1),
-    ('V', 'outc', 'x', 0, 1, 0),
-    ('P', 'dxB', 0, 2, 'k0'),
-    ('P', 'dxB', 0, 2, 'k1'),
-    ('V', 'outc', 'x', 0, 1, 1),
-    ('V', 'quantB', 'k11'),
-    ('D', 'store', 'x', 0, 0),
-    ('P', 'dxB', 0, 3, 'k0'),
-    ('V', 'outc', 'x', 0, 2, 0),
-    ('P', 'dxB', 0, 3, 'k1'),
-    ('V', 'outc', 'x', 0, 2, 1),
-    ('P', 'dw', 'k', '1', 0),
-    ('V', 'outc', 'x', 0, 3, 0),
-    ('V', 'outc', 'x', 0, 3, 1),
-    ('P', 'dw', 'k', '1', 1),
-    ('V', 'outc', 'w', 'k', '1', 0, 1),
-    ('S', 'outc', 'w', 'k', '1', 0, 0),
-    ('D', 'store', 'x', 0, 1),
-    ('P', 'dw', 'k', '1', 2),
-    ('V', 'outc', 'w', 'k', '1', 1, 1),
-    ('S', 'outc', 'w', 'k', '1', 1, 0),
-    ('D', 'store', 'w', 'k', '1', 0),
-    ('P', 'dw', 'k', '1', 3),
-    ('V', 'outc', 'w', 'k', '1', 2, 1),
-    ('S', 'outc', 'w', 'k', '1', 2, 0),
-    ('P', 'dxB', 1, 0, 'q0,q1,k0'),
-    ('V', 'outc', 'w', 'k', '1', 3, 1),
-    ('S', 'outc', 'w', 'k', '1', 3, 0),
-    ('D', 'store', 'w', 'k', '1', 1),
-    ('P', 'dxB', 1, 0, 'k1'),
-    ('P', 'dxB', 1, 1, 'q0,q1,k0'),
-    ('V', 'outc', 'x', 1, 0, 0),
-    ('V', 'outc', 'x', 1, 0, 1),
-    ('P', 'dxB', 1, 1, 'k1'),
-    ('P', 'dxB', 1, 2, 'q0,q1,k0'),
-    ('V', 'outc', 'x', 1, 1, 0),
-    ('V', 'outc', 'x', 1, 1, 1),
-    ('D', 'store', 'x', 1, 0),
-    ('P', 'dxB', 1, 2, 'k1'),
-    ('P', 'dxB', 1, 3, 'q0,q1,k0'),
-    ('V', 'outc', 'x', 1, 2, 0),
-    ('V', 'outc', 'x', 1, 2, 1),
-    ('P', 'dxB', 1, 3, 'k1'),
-    ('V', 'outc', 'x', 1, 3, 0),
-    ('V', 'outc', 'x', 1, 3, 1),
-    ('D', 'store', 'x', 1, 1),
-]
+BANK = 512
+TENSORS = "qkv"
+
+STAGES = {"A": ("v0", "v1", "q0", "q1"), "B": ("k0", "k1")}
+
+ORDER = """
+D load rope; D load q01; D load v00; S table cos; V table sin; D load i0; V mult q01 0; D load q11; P turn v00;
+S group v00 0; V add q01 0; D load i1; S group v00 1; V mult q01 1; S group i0 0; D load v10; S group_features v00 0;
+V quant_tokens v00; S group i0 1; V add q01 1; D load w4; S group_features v00 1; V mult q11 0; P turn q01;
+S group i0 2; D load v01; S group_features q01 0; V quant i0 1; S group i1 0; P turn v10; V add q11 0; D load q00;
+V mult q11 1; S group_features q01 1; D load q10; S group v10 0; S group_features v10 0; V quant_tokens q01;
+D load v11; S group i1 1; P turn v01; V add q11 1; S group v10 1; V quant_features q01; D load w5;
+V quant_features v00; V quant i1 0; S group i1 2; V quant_tokens q11; V quant i0 0; S group w4 0; D load w1;
+V quant i1 1; V quant_tokens v10; P dw q 1 0; S group_features v01 0; V mult q00 0; S group_features v10 1;
+P dw q 1 1; S group w4 1; P turn q11; S dw_out q 1 1 1; V mult q10 0; S group_features v01 1; S group w4 2;
+P dw v 0 0; S group_features q11 0; V quant_features v01; V add q10 0; S dw_out q 1 0 0; P turn v11;
+S dw_out v 0 0 0; S dw_out v 0 0 1; V add q00 0; D dw_store v 0 0; S dw_out q 1 1 0; P dw v 0 1; S group v01 0;
+D dw_store q 1 1; V mult q00 1; P dw q 1 2; D load w0; S group_features v11 0; S group w1 0; V quant w4 0;
+S dw_out v 0 1 0; V add q00 1; S dw_out q 1 0 1; S dw_out q 1 2 0; P dw q 1 3; S dw_out v 0 1 1; V mult q10 1;
+D dw_store v 0 1; S group w5 0; P dw v 0 2; D load k11; S dw_out q 1 3 0; S dw_out q 1 3 1; S group_features q11 1;
+P dw v 0 3; V quant_tokens q00; D load k10; V add q10 1; S group w5 1; P turn q00; D dw_store q 1 3;
+V quant_features v10; S dw_out v 0 2 1; V quant_tokens q10; S dw_out v 0 2 0; V dw_out v 0 3 0; D dw_store v 0 2;
+S dw_out v 0 3 1; P dw q 0 0; S group_features v11 1; V quant w5 0; S group v01 1; D dw_store q 1 0;
+V dw_out q 1 2 1; V group w0 0; P dw q 0 1; D load k00; V quant_features v11; S group_features q00 0; V quant w4 1;
+P dx A 1 m 1 v0,v1; V mult k10 0; D dw_store q 1 2; S dw_out q 0 1 1; P turn q10; S dw_out q 0 0 1; S group w0 1;
+D load k01; P dw q 0 2; S group_features q00 1; V dw_out q 0 1 0; V quant_tokens v01; S group w1 1;
+V quant_features q11; V dw_out q 0 2 1; V quant w0 0; P dw q 0 3; S dw_out q 0 2 0; V quant_features q00;
+S group w5 2; V add k10 0; P dx A 0 m 3 v0,v1,q0; S dw_out q 0 3 0; D load w2; V quant w1 0; S dw_out q 0 0 0;
+P dx A 0 m 0 v0,v1,q0; V mult k10 1; S group_features q10 0; P dx A 0 m 0 q1; P dx A 0 m 3 q1; P dx A 0 m 1 v0,v1,q0;
+S dw_out q 0 3 1; S group_features q10 1; P dx A 0 m 2 v0,v1,q0; V quant w5 1; S dx_out 0 m 3; V add k10 1;
+P dx A 0 m 1 q1; S group w1 2; P dx A 0 m 2 q1; V quant_features q10; P turn k10; S group w0 2; V mult k00 0;
+D load w3; P dx A 1 m 0 v0,v1; S dx_out 0 m 0; S dx_out 0 m 2; P dx A 1 m 1 q0,q1; D dw_store q 0 2; S group w2 0;
+P dx A 1 m 0 q0,q1; V quant w0 1; V quant w1 1; P dx A 0 t 1 v0,v1,q0; D dw_store q 0 1; V mult k00 1; S group v11 0;
+P dx A 0 t 1 q1; P dx A 1 t 1 v0,v1; S dx_out 1 m 0; P dx A 1 t 1 q0,q1; S dx_out 1 m 1; P dx A 1 t 0 v0,v1;
+V add k00 0; S dx_out 1 t 1; P dx A 1 m 2 v0,v1; S group w3 0; P dx A 0 t 0 v0,v1,q0; V quant_tokens k10;
+V add k00 1; P dx A 1 m 2 q0,q1; S group_features k10 0; P dx A 1 t 0 q0,q1; V mult k01 0; P dx A 0 t 0 q1;
+S dx_out 1 m 2; P turn k00; S group v11 1; S dx_out 0 m 1; V quant_tokens k00; S dx_out 1 t 0; V quant_tokens v11;
+P dw k 0 0; S group_features k00 0; V add k01 0; P dx A 1 m 3 v0,v1; S dw_out k 0 0 1; V mult k11 0;
+S dw_out k 0 0 0; P dx A 1 m 3 q0,q1; D dw_store k 0 0; S dx_out 0 t 1; P dw k 0 1; S dx_out 1 m 3; D dw_store q 0 0;
+S dx_out 0 t 0; P dw v 1 0; V mult k01 1; S dw_out k 0 1 0; D dw_store v 0 3; S group_features k00 1; P dw v 1 1;
+S dw_out k 0 1 1; S dw_out v 1 0 1; S dw_out v 1 0 0; P dw v 1 2; V add k11 0; D dw_store v 1 0; S dw_out v 1 1 0;
+S dw_out v 1 1 1; P dw k 0 2; V add k01 1; S group_features k10 1; D dw_store v 1 1; D dw_store q 0 3; V mult k11 1;
+S dw_out v 1 2 1; P turn k01; S group w3 1; P dw k 0 3; S dw_out k 0 2 0; S dw_out k 0 2 1; D dw_store k 0 2;
+S group_features k01 0; V add k11 1; P dw v 1 3; S dw_out v 1 2 0; V quant_tokens k01; D dw_store v 1 2;
+S dw_out k 0 3 0; P turn k11; V quant_tokens k11; S dw_out v 1 3 1; V group w2 1; S group_features k01 1; P dw k 1 0;
+V quant w3 0; S dw_out v 1 3 0; V quant_features k00; D dw_store v 1 3; S dw_out k 0 3 1; V quant w2 0; S group w3 2;
+P dw k 1 1; V quant_features k01; D dw_store k 0 1; V group w2 2; P dx B 0 m 1 k0,k1; D dw_store k 0 3;
+S dw_out k 1 1 1; S dw_out k 1 0 0; V quant w2 1; P dx B 0 m 0 k0,k1; V quant w3 1; S dw_out k 1 1 0;
+V quant_features k10; P dx B 0 m 3 k0,k1; D dw_store k 1 1; S group_features k11 0; V dx_add 0 m 1;
+P dx B 0 t 1 k0,k1; V dx_add 0 m 0; P dx B 0 t 0 k0,k1; S dw_out k 1 0 1; V dx_add 0 t 1; D dw_store k 1 0;
+S group_features k11 1; P dx B 0 m 2 k0,k1; V dx_add 0 t 0; P dx_turn 0 1; V quant_features k11; P dx_turn 0 0;
+P dw k 1 2; V dx_tail 0 1 0; S dx_tail 0 0 1; V dx_tail 0 0 0; S dx_tail 0 1 1; D dx_store 0 0; V dx_add 0 m 2;
+V dx_add 0 m 3; P dx B 1 m 0 k0,k1; S dw_out k 1 2 0; P dx B 1 t 0 k0,k1; S dw_out k 1 2 1; V dx_add 1 m 0;
+D dx_store 0 1; P dx B 1 t 1 k0,k1; V dx_add 1 t 0; P dx B 1 m 1 k0,k1; V dx_add 1 t 1; P dx_turn 1 0;
+V dx_add 1 m 1; D dw_store k 1 2; P dx_turn 1 1; V dx_tail 1 0 0; P dx B 1 m 3 k0,k1; S dx_tail 1 1 0;
+D dx_store 1 0; S dx_tail 1 0 1; S dx_tail 1 1 1; P dx B 1 m 2 k0,k1; V dx_add 1 m 3; P dw k 1 3; V dx_add 1 m 2;
+D dx_store 1 1; S dw_out k 1 3 0; V dw_out k 1 3 1; D dw_store k 1 3
+"""
 
 
 def tile_jointattention_pa_v_kernel(tc, img, rope, W_img_qkv, grad_0, grad_1, grad_2, out_0, out_1):
     nc = tc.nc
-    names = "qkv"
-    grads = {n: a.rearrange("b (s h) (g p j) d -> b s g p h (j d)", s=2, g=2, p=P, j=4) for n, a in zip(names, (grad_0, grad_1, grad_2))}
-    img_v = img.rearrange("b (g p j) c -> b g p j c", g=2, p=P, j=4)
-    w_v = W_img_qkv.rearrange("(s p j) c -> s p j c", s=6, p=P, j=4)
-    rope_v = rope.rearrange("b (g p j) d -> b p g (j d)", g=2, p=P, j=4)
-    out0_v = out_0.rearrange("b (g p j) c -> b g p j c", g=2, p=P, j=4)
-    out1_v = out_1.rearrange("(s m t) c -> s m t c", s=6, m=P, t=4)
+
+    grad_qk = {x: a.rearrange("b (s h) (g p j) d -> b s g p h (j d)", s=2, g=2, p=P, j=4) for x, a in (("q", grad_0), ("k", grad_1))}
+    grad_v = grad_2.rearrange("b (s h) (g p j) d -> b s g h p j d", s=2, g=2, p=P, j=4)
+    img_rows = img.rearrange("b (g p j) c -> b g p j c", g=2, p=P, j=4)
+    w_rows = W_img_qkv.rearrange("(n p j) c -> n p j c", n=6, p=P, j=4)
+    rope_rows = rope.rearrange("b (g p j) d -> b p g (j d)", g=2, p=P, j=4)
+    out_0_rows = out_0.rearrange("b (g p j) c -> b g p j c", g=2, p=P, j=4)
+    out_1_by_four = out_1.rearrange("(n m t) c -> n t m c", n=6, m=P, t=4)
+    out_1_by_head = out_1.rearrange("(n t m) c -> n t m c", n=6, m=P, t=4)
 
     with ExitStack() as ctx:
         const = ctx.enter_context(tc.tile_pool(name="const", bufs=1))
-        gpool = ctx.enter_context(tc.tile_pool(name="gpool", bufs=7))
-        raw = ctx.enter_context(tc.tile_pool(name="raw", bufs=3))
-        inter = ctx.enter_context(tc.tile_pool(name="inter", bufs=3))
-        prod = ctx.enter_context(tc.tile_pool(name="prod", bufs=3))
-        dyp = ctx.enter_context(tc.tile_pool(name="dyp", bufs=3))
-        apool = ctx.enter_context(tc.tile_pool(name="apool", bufs=8))
-        bpool = ctx.enter_context(tc.tile_pool(name="bpool", bufs=10))
-        outp = ctx.enter_context(tc.tile_pool(name="outp", bufs=8))
-        tabp = ctx.enter_context(tc.psum_pool(name="tabp", bufs=1))
-        tpp = ctx.enter_context(tc.psum_pool(name="tpp", bufs=2))
-        accp = ctx.enter_context(tc.psum_pool(name="accp", bufs=4))
+        grad_pool = ctx.enter_context(tc.tile_pool(name="grad", bufs=7))
+        row_pool = ctx.enter_context(tc.tile_pool(name="rows", bufs=3))
+        grouped_pool = ctx.enter_context(tc.tile_pool(name="grouped", bufs=3))
+        product_pool = ctx.enter_context(tc.tile_pool(name="products", bufs=3))
+        dy_pool = ctx.enter_context(tc.tile_pool(name="dy", bufs=3))
+        token_pool = ctx.enter_context(tc.tile_pool(name="token_codes", bufs=8))
+        feature_pool = ctx.enter_context(tc.tile_pool(name="feature_codes", bufs=10))
+        tail_pool = ctx.enter_context(tc.tile_pool(name="tails", bufs=4))
+        dw_pool = ctx.enter_context(tc.tile_pool(name="dw_rows", bufs=5))
+        dx_pool = ctx.enter_context(tc.tile_pool(name="dx_rows", bufs=4))
+        turn_psum = ctx.enter_context(tc.psum_pool(name="turned", bufs=3))
+        sum_psum = ctx.enter_context(tc.psum_pool(name="sums", bufs=5))
         ctx.enter_context(tc.manual_schedule())
 
-        ident = const.tile([P, P], F32)
-        ident_bf = const.tile([P, P], BF16)
+        identity = const.tile([P, P], F32)
         rope_sb = const.tile([P, 2, 512], BF16)
+        tables = {}
+        for part in ("cos", "sin"):
+            table_tile = const.tile([P, 2, P, 4], BF16, name=part)
+            tables[part] = table_tile
         w_codes = const.tile([P, 6, HID], U32, align_bytes=64)
         w_scales = const.tile([P, 6, HID], U8, align_bytes=64)
-        i_codes = const.tile([P, 2, HID], U32, align_bytes=64)
-        i_scales = const.tile([P, 2, HID], U8, align_bytes=64)
+        img_codes = const.tile([P, 2, HID], U32, align_bytes=64)
+        img_scales = const.tile([P, 2, HID], U8, align_bytes=64)
+        make_identity(nc, identity[:])
         live = {}
-        make_identity(nc, ident_bf[:])
-        make_identity(nc, ident[:])
 
         def copy(engine, out, in_):
             if engine == "V":
                 nc.vector.tensor_copy(out=out, in_=in_)
-            elif engine == "S":
+            else:
                 nc.scalar.copy(out=out, in_=in_)
 
-        def load(engine, u):
-            if u == "rope":
-                nc.sync.dma_start(out=rope_sb[:], in_=rope_v[0])
-            elif u[0] == "i":
-                rtile = raw.tile([P, 4, HID], BF16, align_bytes=64)
-                nc.sync.dma_start(out=rtile[:], in_=img_v[0, int(u[1])])
-                live["raw", u] = rtile
-            elif u[0] == "w":
-                rtile = raw.tile([P, 4, HID], BF16, align_bytes=64)
-                nc.sync.dma_start(out=rtile[:], in_=w_v[int(u[1])])
-                live["raw", u] = rtile
+        def load(engine, name):
+            if name == "rope":
+                nc.sync.dma_start(out=rope_sb[:], in_=rope_rows[0])
+            elif name[0] in "iw":
+                rows = row_pool.tile([P, 4, HID], BF16, align_bytes=64)
+                nc.sync.dma_start(out=rows[:], in_=img_rows[0, int(name[1])] if name[0] == "i" else w_rows[int(name[1])])
+                live["rows", name] = rows
             else:
-                gtile = gpool.tile([P, 4, 512], BF16, align_bytes=64)
-                nc.sync.dma_start(out=gtile[:], in_=grads[u[0]][0, int(u[2]), int(u[1])])
-                live["g", u] = gtile
+                x, g, s = name[0], int(name[1]), int(name[2])
+                grad = grad_pool.tile([P, 4 * 4 * P], BF16, align_bytes=64)
+                live["grad", name] = grad
+                if x == "v":
+                    by_token = grad[:].rearrange("p (j h d) -> p j h d", j=4, h=4)
+                    for h in range(4):
+                        nc.sync.dma_start(out=by_token[:, :, h, :], in_=grad_v[0, s, g, h])
+                else:
+                    nc.sync.dma_start(out=grad[:].rearrange("p (h n) -> p h n", h=4), in_=grad_qk[x][0, s, g])
 
-        def interleave(engine, u, pc):
-            if pc != 1:
-                it = inter.tile([P, 512, 4], BF16, align_bytes=64)
-                live["it", u, pc // 2] = it
-            lo = 256 * (pc % 2)
-            copy(engine, live["it", u, pc // 2][:, lo:lo + 256, :], live["raw", u][:, :, 256 * pc:256 * pc + 256].rearrange("p j w -> p w j"))
+        def group(engine, name, piece):
+            piece = int(piece)
+            if name[0] == "v":
+                if piece == 0:
+                    dy = dy_pool.tile([P, 512, 4], BF16, tag="dy", align_bytes=64)
+                    live["dy", name] = dy
+                out = live["dy", name][:, 256 * piece:256 * piece + 256, :]
+                rows = live["grad", name][:].rearrange("p (j w) -> p j w", j=4)
+            else:
+                if piece != 1:
+                    grouped = grouped_pool.tile([P, 512, 4], BF16, align_bytes=64)
+                    live["grouped", name, piece // 2] = grouped
+                start = 256 * (piece % 2)
+                out = live["grouped", name, piece // 2][:, start:start + 256, :]
+                rows = live["rows", name][:]
+            in_ = rows[:, :, 256 * piece:256 * piece + 256]
+            copy(engine, out.rearrange("p (c i) j -> p c j i", i=4), in_.rearrange("p j (c i) -> p c j i", i=4))
 
-        def quantK(engine, u, part):
-            n = 512 - 256 * part
-            lo = 512 * part
-            codes, scales = (i_codes, i_scales) if u[0] == "i" else (w_codes, w_scales)
+        def quant(engine, name, part):
+            start, width = (0, 512) if part == "0" else (512, 256)
+            codes, scales = (img_codes, img_scales) if name[0] == "i" else (w_codes, w_scales)
             nc.vector.quantize_mx(
-                out=codes[:, int(u[1]), lo:lo + n].bitcast(E4M3),
-                scales=scales[:, int(u[1]), lo:lo + n],
-                in_=live["it", u, part][:, 0:n, :].rearrange("p w j -> p (w j)"),
+                out=codes[:, int(name[1]), start:start + width].bitcast(E4M3),
+                scales=scales[:, int(name[1]), start:start + width],
+                in_=live["grouped", name, int(part)][:, 0:width, :].rearrange("p w j -> p (w j)"),
             )
 
-        def dup(engine, which):
-            pairs = rope_sb[:].rearrange("p g (n e) -> p (g n) e", e=2)
-            d = dyp.tile([P, 512, 2], BF16, tag="dya", align_bytes=64)
-            copy(engine, d[:], pairs[:, :, which:which + 1].to_broadcast([P, 512, 2]))
-            live["dup", which] = d
+        def table(engine, part):
+            for g in range(2):
+                pairs = rope_sb[:, g, :].rearrange("p (j i e) -> p i e j", j=4, e=2)
+                chosen = pairs[:, :, 0:1, :] if part == "cos" else pairs[:, :, 1:2, :]
+                copy(engine, tables[part][:, g].rearrange("p (i e) j -> p i e j", e=2), chosen.to_broadcast([P, 64, 2, 4]))
 
-        def tab1(engine, which):
-            flat = live["dup", which][:].rearrange("p n e -> p (n e)")
-            turned = tpp.tile([P, 8, P], BF16, tag="tp")
-            for b in range(8):
-                nc.tensor.transpose(turned[:, b, :], flat[:, b * P:(b + 1) * P], ident_bf[:])
-            live["turned", which] = turned
-
-        def tabcopy(engine, which):
-            back = dyp.tile([P, 8, P], BF16, tag="dyb", align_bytes=64)
-            copy(engine, back[:], live["turned", which][:])
-            live["back", which] = back
-
-        def tab2(engine, which):
-            table = tabp.tile([P, 8, P], BF16, name="table%d" % which)
-            for b in range(8):
-                nc.tensor.transpose(table[:, b, :], live["back", which][:, b, :], ident_bf[:])
-            live["table", which] = table
-
-        def sortv(engine, u, part):
-            if part == 0:
-                d = dyp.tile([P, 4, P, 4], BF16, tag="dya", align_bytes=64)
-                live["dya", u] = d
-            d = live["dya", u]
-            for h in range(2 * part, 2 * part + 2):
-                copy(
-                    engine,
-                    d[:, :, h * 32:(h + 1) * 32, :].rearrange("p t q j -> p q t j"),
-                    live["g", u][:, h, :].rearrange("p (j q t) -> p q t j", j=4, t=4),
+        def mult(engine, unit, half):
+            g, half = int(unit[1]), int(half)
+            grad = live["grad", unit][:, 1024 * half:1024 * half + 1024].rearrange("p (h j d) -> p h d j", h=2, j=4)
+            for part in ("cos", "sin"):
+                product = product_pool.tile([P, 2, P, 4], F32, tag=part, align_bytes=64)
+                live[part, unit, half] = product
+                nc.vector.tensor_tensor(
+                    out=product[:], in0=grad, in1=tables[part][:, g:g + 1, :, :].to_broadcast([P, 2, P, 4]), op=mybir.AluOpType.mult
                 )
 
-        def mult(engine, u, part):
-            g = int(u[1])
-            for which in range(2):
-                pt = prod.tile([P, 4, 64, 4], F32, name="prod%d" % which, align_bytes=64)
-                live["prod", u, part, which] = pt
-            for hh in range(2):
-                for which in range(2):
-                    nc.vector.tensor_tensor(
-                        out=live["prod", u, part, which][:, :, hh * 32:(hh + 1) * 32, :].rearrange("p t q j -> p q t j"),
-                        in0=live["g", u][:, 2 * part + hh, :].rearrange("p (j q t) -> p q t j", j=4, t=4),
-                        in1=live["table", which][:, 4 * g:4 * g + 4, :].rearrange("p j (q t) -> p q t j", t=4),
-                        op=MUL,
-                    )
+        def add(engine, unit, half):
+            half = int(half)
+            if half == 0:
+                dy = dy_pool.tile([P, 4, P, 4], BF16, tag="dy", align_bytes=64)
+                live["dy", unit] = dy
+            out = live["dy", unit][:].rearrange("p (a e) m j -> p a e m j", e=2)
+            cos, sin = [live[part, unit, half][:].rearrange("p h (q a e) j -> p a e (h q) j", a=2, e=2) for part in ("cos", "sin")]
+            for e in range(2):
+                nc.vector.tensor_tensor(
+                    out=out[:, :, e, 64 * half:64 * half + 64, :], in0=cos[:, :, e], in1=sin[:, :, 1 - e],
+                    op=mybir.AluOpType.add if e == 0 else mybir.AluOpType.subtract,
+                )
 
-        def add(engine, u, part, e):
-            if part == 0 and e == 0:
-                d = dyp.tile([P, 4, P, 4], BF16, tag="dya", align_bytes=64)
-                live["dya", u] = d
-            d = live["dya", u][:].rearrange("p (a e) q j -> p a e (q j)", e=2)
-            p0 = live["prod", u, part, 0][:].rearrange("p (a e) q j -> p a e (q j)", e=2)
-            p1 = live["prod", u, part, 1][:].rearrange("p (a e) q j -> p a e (q j)", e=2)
-            eng = nc.gpsimd if engine == "G" else nc.vector
-            eng.tensor_tensor(
-                out=d[:, :, e, part * 256:(part + 1) * 256], in0=p0[:, :, e, :], in1=p1[:, :, 1 - e, :], op=ADD if e == 0 else SUB
-            )
+        def quant_tokens(engine, unit):
+            codes = token_pool.tile([P, 512], U32, align_bytes=64)
+            scales = token_pool.tile([P, 512], U8, align_bytes=64)
+            dy = live["dy", unit][:].rearrange("p w j -> p (w j)" if unit[0] == "v" else "p t m j -> p (t m j)")
+            nc.vector.quantize_mx(out=codes[:].bitcast(E5M2), scales=scales[:], in_=dy)
+            live["tokens", unit] = (codes, scales)
 
-        def quantA(engine, u):
-            ac = apool.tile([P, 512], U32, align_bytes=64)
-            asc = apool.tile([P, 512], U8, align_bytes=64)
-            nc.vector.quantize_mx(out=ac[:].bitcast(E5M2), scales=asc[:], in_=live["dya", u][:].rearrange("p t q j -> p (t q j)"))
-            live["A", u] = (ac, asc)
+        def turn(engine, unit):
+            source = live["grad", unit][:] if unit[0] == "v" else live["dy", unit][:].rearrange("p t m j -> p (t m j)")
+            words = source.bitcast(F32)
+            for r in range(2):
+                bank = turn_psum.tile([P, 4, P], F32, tag="turned")
+                for n in range(4):
+                    first = 256 * (2 * r + n // 2) + n % 2 if unit[0] == "v" else 256 * n + r
+                    nc.tensor.transpose(bank[:, n, :], words[:, first:first - first % 2 + 256:2], identity[:])
+                live["turned", unit, r] = bank
 
-        def turn(engine, u, pair):
-            words = live["dya", u][:].rearrange("p t q j -> p (t q j)").bitcast(F32)
-            tp = tpp.tile([P, 4, P], F32, tag="tp")
-            for t in range(4):
-                nc.tensor.transpose(tp[:, t, :], words[:, t * 256 + pair:(t + 1) * 256:2], ident[:])
-            live["tp", u, pair] = tp
+        def group_features(engine, unit, r):
+            r = int(r)
+            if r == 0:
+                dy_t = dy_pool.tile([P, 2, 1024], BF16, tag="dy_t", align_bytes=64)
+                live["dy_t", unit] = dy_t
+            out = live["dy_t", unit][:, r, :]
+            bank = live["turned", unit, r][:]
+            if unit[0] == "v":
+                copy(engine, out.bitcast(F32).rearrange("p (j c u) -> p j c u", j=2, u=2), bank.rearrange("p (j u) c -> p j c u", j=2))
+            else:
+                pairs = bank.rearrange("p t c -> p (t c)").bitcast(BF16)
+                copy(engine, out.rearrange("p (e c t) -> p e c t", e=2, t=4), pairs.rearrange("p (t c e) -> p e c t", t=4, e=2))
 
-        def copyB(engine, u, pair):
-            if pair == 0:
-                db = dyp.tile([P, 2, 1024], BF16, tag="dyb", align_bytes=64)
-                live["dyb", u] = db
-            copy(
-                engine,
-                live["dyb", u][:, pair, :].rearrange("p (e c t) -> p e c t", e=2, t=4),
-                live["tp", u, pair][:].rearrange("p t c -> p (t c)").bitcast(BF16).rearrange("p (t c e) -> p e c t", t=4, e=2),
-            )
-
-        def quantB(engine, u):
-            bc = bpool.tile([P, 512], U32, align_bytes=64)
-            bsc = bpool.tile([P, 512], U8, align_bytes=64)
-            nc.vector.quantize_mx(out=bc[:].bitcast(E5M2), scales=bsc[:], in_=live["dyb", u][:].rearrange("p u c -> p (u c)"))
-            live["B", u] = (bc, bsc)
-
-        def mm(key, half, lhs, cols, rhs, n, start, stop):
-            codes, scales = lhs
-            rc, rs = rhs
-            c = slice(256 * half, 256 * half + 512)
-            nc.tensor.matmul_mx(
-                out=live["acc", key, half][:], lhsT=codes[:, cols].bitcast(E5M2), lhsT_scale=scales[:, cols],
-                rhs=rc[:, n, c].bitcast(E4M3), rhs_scale=rs[:, n, c], start=start, stop=stop,
-            )
-
-        def open_acc(key):
-            for half in range(2):
-                acc = accp.tile([P, 512], F32)
-                live["acc", key, half] = acc
+        def quant_features(engine, unit):
+            codes = feature_pool.tile([P, 512], U32, align_bytes=64)
+            scales = feature_pool.tile([P, 512], U8, align_bytes=64)
+            nc.vector.quantize_mx(out=codes[:].bitcast(E5M2), scales=scales[:], in_=live["dy_t", unit][:].rearrange("p r c -> p (r c)"))
+            live["features", unit] = (codes, scales)
 
         def dw(engine, x, s, t):
-            key = ("w", x, s, t)
-            open_acc(key)
+            cols = slice(P * int(t), P * int(t) + P)
+            for part in range(2):
+                total = sum_psum.tile([P, BANK], F32, tag="sum")
+                live["dw", x, s, t, part] = total
             for g in range(2):
-                for half in range(2):
-                    mm(key, half, live["A", "%s%d%s" % (x, g, s)], slice(t * P, (t + 1) * P), (i_codes, i_scales), g, g == 0, g == 1)
+                codes, scales = live["tokens", "%s%d%s" % (x, g, s)]
+                for part in range(2):
+                    img_cols = slice(256 * part, 256 * part + BANK)
+                    nc.tensor.matmul_mx(
+                        out=live["dw", x, s, t, part][:],
+                        lhsT=codes[:, cols].bitcast(E5M2), lhsT_scale=scales[:, cols],
+                        rhs=img_codes[:, g, img_cols].bitcast(E4M3), rhs_scale=img_scales[:, g, img_cols],
+                        start=(g == 0), stop=(g == 1),
+                    )
 
-        STAGE = {('A', 0): ['v0', 'v1', 'q0', 'q1'], ('A', 1): ['v0', 'v1'], ('B', 0): ['k0', 'k1'], ('B', 1): ['q0', 'q1', 'k0', 'k1']}
-
-        def dx(stage, g, j, units):
-            key = ("x" + stage, g, j)
-            members = STAGE[stage, g]
-            for u in units.split(","):
-                if u == members[0]:
-                    open_acc(key)
-                for half in range(2):
-                    mm(key, half, live["B", "%s%s%s" % (u[0], g, u[1])], slice(j * P, (j + 1) * P), (w_codes, w_scales),
-                       2 * names.index(u[0]) + int(u[1]), u == members[0], u == members[-1])
-
-        def result(group):
-            if ("res", group) not in live:
-                res = outp.tile([P, 2, HID], F32)
-                live["res", group] = res
-            return live["res", group]
-
-        def halves(key, pos, group, half):
-            a = live["acc", key, half]
-            res = result(group)
-            if half == 0:
-                return res[:, pos % 2, 0:512], a[:]
-            return res[:, pos % 2, 512:768], a[:, 256:512]
-
-        def outA(engine, x, g, j, half):
-            out, in_ = halves(("xA", g, j), j, ("x", g, j // 2), half)
-            copy(engine, out, in_)
-
-        def outc(engine, *key):
-            half = key[-1]
-            pos = key[-2]
-            group = key[:-2] + (pos // 2,)
-            if key[0] == "w":
-                out, in_ = halves(key[:-1], pos, group, half)
-                copy(engine, out, in_)
+        def dw_out(engine, x, s, t, part):
+            part = int(part)
+            if ("dw_rows", x, s, t) not in live:
+                rows = dw_pool.tile([P, HID], F32)
+                live["dw_rows", x, s, t] = rows
+            total = live["dw", x, s, t, part]
+            if part == 0:
+                copy(engine, live["dw_rows", x, s, t][:, 0:512], total[:])
             else:
-                out, in_ = halves(("xB",) + key[1:-1], pos, group, half)
-                nc.vector.tensor_tensor(out=out, in0=in_, in1=out, op=ADD)
+                copy(engine, live["dw_rows", x, s, t][:, 512:768], total[:, 256:512])
 
-        def store(engine, *key):
-            th = key[-1]
-            if key[0] == "w":
-                dst = out1_v[2 * names.index(key[1]) + int(key[2]), :, 2 * th:2 * th + 2, :]
-            else:
-                dst = out0_v[0, key[1], :, 2 * th:2 * th + 2, :]
-            nc.sync.dma_start(out=dst, in_=live["res", key][:])
+        def dw_store(engine, x, s, t):
+            view = out_1_by_head if x == "v" else out_1_by_four
+            nc.sync.dma_start(out=view[2 * TENSORS.index(x) + int(s), int(t)], in_=live["dw_rows", x, s, t][:])
 
-        RUN = {"load": load, "interleave": interleave, "quantK": quantK, "dup": dup, "tab1": tab1, "tabcopy": tabcopy, "tab2": tab2, "sortv": sortv,
-               "mult": mult, "add": add, "quantA": quantA, "turn": turn, "copyB": copyB, "quantB": quantB, "dw": dw,
-               "dxA": lambda e, *a: dx("A", *a), "dxB": lambda e, *a: dx("B", *a), "outA": outA, "outc": outc, "store": store}
-        for step in SCHEDULE:
-            RUN[step[1]](step[0], *step[2:])
+        def dx(engine, stage, g, form, n, members):
+            for member in members.split(","):
+                if member == STAGES[stage][0]:
+                    total = sum_psum.tile([P, BANK], F32, tag="sum")
+                    live["dx", stage, g, form, n] = total
+                codes, scales = live["features", member[0] + g + member[1]]
+                k = 2 * TENSORS.index(member[0]) + int(member[1])
+                if form == "m":
+                    cols = slice(P * int(n), P * int(n) + P)
+                    lhs, lhs_scale = codes[:, cols].bitcast(E5M2), scales[:, cols]
+                    rhs, rhs_scale = w_codes[:, k, 0:BANK].bitcast(E4M3), w_scales[:, k, 0:BANK]
+                else:
+                    cols = slice(BANK + P * int(n), BANK + P * int(n) + P)
+                    lhs, lhs_scale = w_codes[:, k, cols].bitcast(E4M3), w_scales[:, k, cols]
+                    rhs, rhs_scale = codes[:].bitcast(E5M2), scales[:]
+                nc.tensor.matmul_mx(
+                    out=live["dx", stage, g, form, n][:], lhsT=lhs, lhsT_scale=lhs_scale, rhs=rhs, rhs_scale=rhs_scale,
+                    start=(member == STAGES[stage][0]), stop=(member == STAGES[stage][-1]),
+                )
+
+        def dx_rows(g, pair):
+            if ("dx_rows", g, pair) not in live:
+                rows = dx_pool.tile([P, 2, HID], F32)
+                live["dx_rows", g, pair] = rows
+            return live["dx_rows", g, pair]
+
+        def dx_place(g, form, n):
+            if form == "m":
+                return dx_rows(g, int(n) // 2)[:, int(n) % 2, 0:BANK]
+            if ("tail", g, n) not in live:
+                tail = tail_pool.tile([P, BANK], F32)
+                live["tail", g, n] = tail
+            return live["tail", g, n][:]
+
+        def dx_out(engine, g, form, n):
+            copy(engine, dx_place(g, form, n), live["dx", "A", g, form, n][:])
+
+        def dx_add(engine, g, form, n):
+            place = dx_place(g, form, n)
+            nc.vector.tensor_tensor(out=place, in0=live["dx", "B", g, form, n][:], in1=place, op=mybir.AluOpType.add)
+
+        def dx_turn(engine, g, n):
+            bank = turn_psum.tile([P, 4, P], F32, tag="turned")
+            for j in range(4):
+                nc.tensor.transpose(bank[:, j, :], live["tail", g, n][:, P * j:P * j + P], identity[:])
+            live["tail_turned", g, n] = bank
+
+        def dx_tail(engine, g, n, pair):
+            start = BANK + P * int(n)
+            j = 2 * int(pair)
+            copy(engine, dx_rows(g, int(pair))[:, :, start:start + P], live["tail_turned", g, n][:, j:j + 2, :])
+
+        def dx_store(engine, g, pair):
+            j = 2 * int(pair)
+            nc.sync.dma_start(out=out_0_rows[0, int(g), :, j:j + 2, :], in_=live["dx_rows", g, int(pair)][:])
+
+        run = {
+            "load": load, "group": group, "quant": quant, "table": table, "mult": mult, "add": add,
+            "quant_tokens": quant_tokens, "turn": turn, "group_features": group_features, "quant_features": quant_features,
+            "dw": dw, "dw_out": dw_out, "dw_store": dw_store,
+            "dx": dx, "dx_out": dx_out, "dx_add": dx_add, "dx_turn": dx_turn, "dx_tail": dx_tail, "dx_store": dx_store,
+        }
+        for line in ORDER.split(";"):
+            engine, name, *arguments = line.split()
+            run[name](engine, *arguments)

from contextlib import ExitStack

import concourse.mybir as mybir
from concourse.masks import make_identity

TOKENS, HID, FEATURES = 1024, 768, 3072
FLOPS = 2 * 2 * TOKENS * FEATURES * HID

F32 = mybir.dt.float32
BF16 = mybir.dt.bfloat16
U32 = mybir.dt.uint32
U8 = mybir.dt.uint8
E4M3 = mybir.dt.float8_e4m3fn_x4
E5M2 = mybir.dt.float8_e5m2_x4

P = 128
BANK = 512
TENSORS = "qkv"

STAGES = {"A": ("v0", "v1", "q0", "q1"), "B": ("k0", "k1")}

ORDER = """
D load rope; D load q01; D load v00; S table cos; V table sin; D load i0; V mult q01 0; D load q11; P turn v00;
S group v00 0; V add q01 0; D load i1; S group v00 1; V mult q01 1; S group i0 0; D load v10; S group_features v00 0;
V quant_tokens v00; S group i0 1; V add q01 1; D load w4; S group_features v00 1; V mult q11 0; P turn q01;
S group i0 2; D load v01; S group_features q01 0; V quant i0 1; S group i1 0; P turn v10; V add q11 0; D load q00;
V mult q11 1; S group_features q01 1; D load q10; S group v10 0; S group_features v10 0; V quant_tokens q01;
D load v11; S group i1 1; P turn v01; V add q11 1; S group v10 1; V quant_features q01; D load w5;
V quant_features v00; V quant i1 0; S group i1 2; V quant_tokens q11; V quant i0 0; S group w4 0; D load w1;
V quant i1 1; V quant_tokens v10; P dw q 1 0; S group_features v01 0; V mult q00 0; S group_features v10 1;
P dw q 1 1; S group w4 1; P turn q11; S dw_out q 1 1 1; V mult q10 0; S group_features v01 1; S group w4 2;
P dw v 0 0; S group_features q11 0; V quant_features v01; V add q10 0; S dw_out q 1 0 0; P turn v11;
S dw_out v 0 0 0; S dw_out v 0 0 1; V add q00 0; D dw_store v 0 0; S dw_out q 1 1 0; P dw v 0 1; S group v01 0;
D dw_store q 1 1; V mult q00 1; P dw q 1 2; D load w0; S group_features v11 0; S group w1 0; V quant w4 0;
S dw_out v 0 1 0; V add q00 1; S dw_out q 1 0 1; S dw_out q 1 2 0; P dw q 1 3; S dw_out v 0 1 1; V mult q10 1;
D dw_store v 0 1; S group w5 0; P dw v 0 2; D load k11; S dw_out q 1 3 0; S dw_out q 1 3 1; S group_features q11 1;
P dw v 0 3; V quant_tokens q00; D load k10; V add q10 1; S group w5 1; P turn q00; D dw_store q 1 3;
V quant_features v10; S dw_out v 0 2 1; V quant_tokens q10; S dw_out v 0 2 0; V dw_out v 0 3 0; D dw_store v 0 2;
S dw_out v 0 3 1; P dw q 0 0; S group_features v11 1; V quant w5 0; S group v01 1; D dw_store q 1 0;
V dw_out q 1 2 1; V group w0 0; P dw q 0 1; D load k00; V quant_features v11; S group_features q00 0; V quant w4 1;
P dx A 1 m 1 v0,v1; V mult k10 0; D dw_store q 1 2; S dw_out q 0 1 1; P turn q10; S dw_out q 0 0 1; S group w0 1;
D load k01; P dw q 0 2; S group_features q00 1; V dw_out q 0 1 0; V quant_tokens v01; S group w1 1;
V quant_features q11; V dw_out q 0 2 1; V quant w0 0; P dw q 0 3; S dw_out q 0 2 0; V quant_features q00;
S group w5 2; V add k10 0; P dx A 0 m 3 v0,v1,q0; S dw_out q 0 3 0; D load w2; V quant w1 0; S dw_out q 0 0 0;
P dx A 0 m 0 v0,v1,q0; V mult k10 1; S group_features q10 0; P dx A 0 m 0 q1; P dx A 0 m 3 q1; P dx A 0 m 1 v0,v1,q0;
S dw_out q 0 3 1; S group_features q10 1; P dx A 0 m 2 v0,v1,q0; V quant w5 1; S dx_out 0 m 3; V add k10 1;
P dx A 0 m 1 q1; S group w1 2; P dx A 0 m 2 q1; V quant_features q10; P turn k10; S group w0 2; V mult k00 0;
D load w3; P dx A 1 m 0 v0,v1; S dx_out 0 m 0; S dx_out 0 m 2; P dx A 1 m 1 q0,q1; D dw_store q 0 2; S group w2 0;
P dx A 1 m 0 q0,q1; V quant w0 1; V quant w1 1; P dx A 0 t 1 v0,v1,q0; D dw_store q 0 1; V mult k00 1; S group v11 0;
P dx A 0 t 1 q1; P dx A 1 t 1 v0,v1; S dx_out 1 m 0; P dx A 1 t 1 q0,q1; S dx_out 1 m 1; P dx A 1 t 0 v0,v1;
V add k00 0; S dx_out 1 t 1; P dx A 1 m 2 v0,v1; S group w3 0; P dx A 0 t 0 v0,v1,q0; V quant_tokens k10;
V add k00 1; P dx A 1 m 2 q0,q1; S group_features k10 0; P dx A 1 t 0 q0,q1; V mult k01 0; P dx A 0 t 0 q1;
S dx_out 1 m 2; P turn k00; S group v11 1; S dx_out 0 m 1; V quant_tokens k00; S dx_out 1 t 0; V quant_tokens v11;
P dw k 0 0; S group_features k00 0; V add k01 0; P dx A 1 m 3 v0,v1; S dw_out k 0 0 1; V mult k11 0;
S dw_out k 0 0 0; P dx A 1 m 3 q0,q1; D dw_store k 0 0; S dx_out 0 t 1; P dw k 0 1; S dx_out 1 m 3; D dw_store q 0 0;
S dx_out 0 t 0; P dw v 1 0; V mult k01 1; S dw_out k 0 1 0; D dw_store v 0 3; S group_features k00 1; P dw v 1 1;
S dw_out k 0 1 1; S dw_out v 1 0 1; S dw_out v 1 0 0; P dw v 1 2; V add k11 0; D dw_store v 1 0; S dw_out v 1 1 0;
S dw_out v 1 1 1; P dw k 0 2; V add k01 1; S group_features k10 1; D dw_store v 1 1; D dw_store q 0 3; V mult k11 1;
S dw_out v 1 2 1; P turn k01; S group w3 1; P dw k 0 3; S dw_out k 0 2 0; S dw_out k 0 2 1; D dw_store k 0 2;
S group_features k01 0; V add k11 1; P dw v 1 3; S dw_out v 1 2 0; V quant_tokens k01; D dw_store v 1 2;
S dw_out k 0 3 0; P turn k11; V quant_tokens k11; S dw_out v 1 3 1; V group w2 1; S group_features k01 1; P dw k 1 0;
V quant w3 0; S dw_out v 1 3 0; V quant_features k00; D dw_store v 1 3; S dw_out k 0 3 1; V quant w2 0; S group w3 2;
P dw k 1 1; V quant_features k01; D dw_store k 0 1; V group w2 2; P dx B 0 m 1 k0,k1; D dw_store k 0 3;
S dw_out k 1 1 1; S dw_out k 1 0 0; V quant w2 1; P dx B 0 m 0 k0,k1; V quant w3 1; S dw_out k 1 1 0;
V quant_features k10; P dx B 0 m 3 k0,k1; D dw_store k 1 1; S group_features k11 0; V dx_add 0 m 1;
P dx B 0 t 1 k0,k1; V dx_add 0 m 0; P dx B 0 t 0 k0,k1; S dw_out k 1 0 1; V dx_add 0 t 1; D dw_store k 1 0;
S group_features k11 1; P dx B 0 m 2 k0,k1; V dx_add 0 t 0; P dx_turn 0 1; V quant_features k11; P dx_turn 0 0;
P dw k 1 2; V dx_tail 0 1 0; S dx_tail 0 0 1; V dx_tail 0 0 0; S dx_tail 0 1 1; D dx_store 0 0; V dx_add 0 m 2;
V dx_add 0 m 3; P dx B 1 m 0 k0,k1; S dw_out k 1 2 0; P dx B 1 t 0 k0,k1; S dw_out k 1 2 1; V dx_add 1 m 0;
D dx_store 0 1; P dx B 1 t 1 k0,k1; V dx_add 1 t 0; P dx B 1 m 1 k0,k1; V dx_add 1 t 1; P dx_turn 1 0;
V dx_add 1 m 1; D dw_store k 1 2; P dx_turn 1 1; V dx_tail 1 0 0; P dx B 1 m 3 k0,k1; S dx_tail 1 1 0;
D dx_store 1 0; S dx_tail 1 0 1; S dx_tail 1 1 1; P dx B 1 m 2 k0,k1; V dx_add 1 m 3; P dw k 1 3; V dx_add 1 m 2;
D dx_store 1 1; S dw_out k 1 3 0; V dw_out k 1 3 1; D dw_store k 1 3
"""


def tile_jointattention_pa_v_kernel(tc, img, rope, W_img_qkv, grad_0, grad_1, grad_2, out_0, out_1):
    nc = tc.nc

    grad_qk = {x: a.rearrange("b (s h) (g p j) d -> b s g p h (j d)", s=2, g=2, p=P, j=4) for x, a in (("q", grad_0), ("k", grad_1))}
    grad_v = grad_2.rearrange("b (s h) (g p j) d -> b s g h p j d", s=2, g=2, p=P, j=4)
    img_rows = img.rearrange("b (g p j) c -> b g p j c", g=2, p=P, j=4)
    w_rows = W_img_qkv.rearrange("(n p j) c -> n p j c", n=6, p=P, j=4)
    rope_rows = rope.rearrange("b (g p j) d -> b p g (j d)", g=2, p=P, j=4)
    out_0_rows = out_0.rearrange("b (g p j) c -> b g p j c", g=2, p=P, j=4)
    out_1_by_four = out_1.rearrange("(n m t) c -> n t m c", n=6, m=P, t=4)
    out_1_by_head = out_1.rearrange("(n t m) c -> n t m c", n=6, m=P, t=4)

    with ExitStack() as ctx:
        const = ctx.enter_context(tc.tile_pool(name="const", bufs=1))
        grad_pool = ctx.enter_context(tc.tile_pool(name="grad", bufs=7))
        row_pool = ctx.enter_context(tc.tile_pool(name="rows", bufs=3))
        grouped_pool = ctx.enter_context(tc.tile_pool(name="grouped", bufs=3))
        product_pool = ctx.enter_context(tc.tile_pool(name="products", bufs=3))
        dy_pool = ctx.enter_context(tc.tile_pool(name="dy", bufs=3))
        token_pool = ctx.enter_context(tc.tile_pool(name="token_codes", bufs=8))
        feature_pool = ctx.enter_context(tc.tile_pool(name="feature_codes", bufs=10))
        tail_pool = ctx.enter_context(tc.tile_pool(name="tails", bufs=4))
        dw_pool = ctx.enter_context(tc.tile_pool(name="dw_rows", bufs=5))
        dx_pool = ctx.enter_context(tc.tile_pool(name="dx_rows", bufs=4))
        turn_psum = ctx.enter_context(tc.psum_pool(name="turned", bufs=3))
        sum_psum = ctx.enter_context(tc.psum_pool(name="sums", bufs=5))
        ctx.enter_context(tc.manual_schedule())

        identity = const.tile([P, P], F32)
        rope_sb = const.tile([P, 2, 512], BF16)
        tables = {}
        for part in ("cos", "sin"):
            table_tile = const.tile([P, 2, P, 4], BF16, name=part)
            tables[part] = table_tile
        w_codes = const.tile([P, 6, HID], U32, align_bytes=64)
        w_scales = const.tile([P, 6, HID], U8, align_bytes=64)
        img_codes = const.tile([P, 2, HID], U32, align_bytes=64)
        img_scales = const.tile([P, 2, HID], U8, align_bytes=64)
        make_identity(nc, identity[:])
        live = {}

        def copy(engine, out, in_):
            if engine == "V":
                nc.vector.tensor_copy(out=out, in_=in_)
            else:
                nc.scalar.copy(out=out, in_=in_)

        def load(engine, name):
            if name == "rope":
                nc.sync.dma_start(out=rope_sb[:], in_=rope_rows[0])
            elif name[0] in "iw":
                rows = row_pool.tile([P, 4, HID], BF16, align_bytes=64)
                nc.sync.dma_start(out=rows[:], in_=img_rows[0, int(name[1])] if name[0] == "i" else w_rows[int(name[1])])
                live["rows", name] = rows
            else:
                x, g, s = name[0], int(name[1]), int(name[2])
                grad = grad_pool.tile([P, 4 * 4 * P], BF16, align_bytes=64)
                live["grad", name] = grad
                if x == "v":
                    by_token = grad[:].rearrange("p (j h d) -> p j h d", j=4, h=4)
                    for h in range(4):
                        nc.sync.dma_start(out=by_token[:, :, h, :], in_=grad_v[0, s, g, h])
                else:
                    nc.sync.dma_start(out=grad[:].rearrange("p (h n) -> p h n", h=4), in_=grad_qk[x][0, s, g])

        def group(engine, name, piece):
            piece = int(piece)
            if name[0] == "v":
                if piece == 0:
                    dy = dy_pool.tile([P, 512, 4], BF16, tag="dy", align_bytes=64)
                    live["dy", name] = dy
                out = live["dy", name][:, 256 * piece:256 * piece + 256, :]
                rows = live["grad", name][:].rearrange("p (j w) -> p j w", j=4)
            else:
                if piece != 1:
                    grouped = grouped_pool.tile([P, 512, 4], BF16, align_bytes=64)
                    live["grouped", name, piece // 2] = grouped
                start = 256 * (piece % 2)
                out = live["grouped", name, piece // 2][:, start:start + 256, :]
                rows = live["rows", name][:]
            in_ = rows[:, :, 256 * piece:256 * piece + 256]
            copy(engine, out.rearrange("p (c i) j -> p c j i", i=4), in_.rearrange("p j (c i) -> p c j i", i=4))

        def quant(engine, name, part):
            start, width = (0, 512) if part == "0" else (512, 256)
            codes, scales = (img_codes, img_scales) if name[0] == "i" else (w_codes, w_scales)
            nc.vector.quantize_mx(
                out=codes[:, int(name[1]), start:start + width].bitcast(E4M3),
                scales=scales[:, int(name[1]), start:start + width],
                in_=live["grouped", name, int(part)][:, 0:width, :].rearrange("p w j -> p (w j)"),
            )

        def table(engine, part):
            for g in range(2):
                pairs = rope_sb[:, g, :].rearrange("p (j i e) -> p i e j", j=4, e=2)
                chosen = pairs[:, :, 0:1, :] if part == "cos" else pairs[:, :, 1:2, :]
                copy(engine, tables[part][:, g].rearrange("p (i e) j -> p i e j", e=2), chosen.to_broadcast([P, 64, 2, 4]))

        def mult(engine, unit, half):
            g, half = int(unit[1]), int(half)
            grad = live["grad", unit][:, 1024 * half:1024 * half + 1024].rearrange("p (h j d) -> p h d j", h=2, j=4)
            for part in ("cos", "sin"):
                product = product_pool.tile([P, 2, P, 4], F32, tag=part, align_bytes=64)
                live[part, unit, half] = product
                nc.vector.tensor_tensor(
                    out=product[:], in0=grad, in1=tables[part][:, g:g + 1, :, :].to_broadcast([P, 2, P, 4]), op=mybir.AluOpType.mult
                )

        def add(engine, unit, half):
            half = int(half)
            if half == 0:
                dy = dy_pool.tile([P, 4, P, 4], BF16, tag="dy", align_bytes=64)
                live["dy", unit] = dy
            out = live["dy", unit][:].rearrange("p (a e) m j -> p a e m j", e=2)
            cos, sin = [live[part, unit, half][:].rearrange("p h (q a e) j -> p a e (h q) j", a=2, e=2) for part in ("cos", "sin")]
            for e in range(2):
                nc.vector.tensor_tensor(
                    out=out[:, :, e, 64 * half:64 * half + 64, :], in0=cos[:, :, e], in1=sin[:, :, 1 - e],
                    op=mybir.AluOpType.add if e == 0 else mybir.AluOpType.subtract,
                )

        def quant_tokens(engine, unit):
            codes = token_pool.tile([P, 512], U32, align_bytes=64)
            scales = token_pool.tile([P, 512], U8, align_bytes=64)
            dy = live["dy", unit][:].rearrange("p w j -> p (w j)" if unit[0] == "v" else "p t m j -> p (t m j)")
            nc.vector.quantize_mx(out=codes[:].bitcast(E5M2), scales=scales[:], in_=dy)
            live["tokens", unit] = (codes, scales)

        def turn(engine, unit):
            source = live["grad", unit][:] if unit[0] == "v" else live["dy", unit][:].rearrange("p t m j -> p (t m j)")
            words = source.bitcast(F32)
            for r in range(2):
                bank = turn_psum.tile([P, 4, P], F32, tag="turned")
                for n in range(4):
                    first = 256 * (2 * r + n // 2) + n % 2 if unit[0] == "v" else 256 * n + r
                    nc.tensor.transpose(bank[:, n, :], words[:, first:first - first % 2 + 256:2], identity[:])
                live["turned", unit, r] = bank

        def group_features(engine, unit, r):
            r = int(r)
            if r == 0:
                dy_t = dy_pool.tile([P, 2, 1024], BF16, tag="dy_t", align_bytes=64)
                live["dy_t", unit] = dy_t
            out = live["dy_t", unit][:, r, :]
            bank = live["turned", unit, r][:]
            if unit[0] == "v":
                copy(engine, out.bitcast(F32).rearrange("p (j c u) -> p j c u", j=2, u=2), bank.rearrange("p (j u) c -> p j c u", j=2))
            else:
                pairs = bank.rearrange("p t c -> p (t c)").bitcast(BF16)
                copy(engine, out.rearrange("p (e c t) -> p e c t", e=2, t=4), pairs.rearrange("p (t c e) -> p e c t", t=4, e=2))

        def quant_features(engine, unit):
            codes = feature_pool.tile([P, 512], U32, align_bytes=64)
            scales = feature_pool.tile([P, 512], U8, align_bytes=64)
            nc.vector.quantize_mx(out=codes[:].bitcast(E5M2), scales=scales[:], in_=live["dy_t", unit][:].rearrange("p r c -> p (r c)"))
            live["features", unit] = (codes, scales)

        def dw(engine, x, s, t):
            cols = slice(P * int(t), P * int(t) + P)
            for part in range(2):
                total = sum_psum.tile([P, BANK], F32, tag="sum")
                live["dw", x, s, t, part] = total
            for g in range(2):
                codes, scales = live["tokens", "%s%d%s" % (x, g, s)]
                for part in range(2):
                    img_cols = slice(256 * part, 256 * part + BANK)
                    nc.tensor.matmul_mx(
                        out=live["dw", x, s, t, part][:],
                        lhsT=codes[:, cols].bitcast(E5M2), lhsT_scale=scales[:, cols],
                        rhs=img_codes[:, g, img_cols].bitcast(E4M3), rhs_scale=img_scales[:, g, img_cols],
                        start=(g == 0), stop=(g == 1),
                    )

        def dw_out(engine, x, s, t, part):
            part = int(part)
            if ("dw_rows", x, s, t) not in live:
                rows = dw_pool.tile([P, HID], F32)
                live["dw_rows", x, s, t] = rows
            total = live["dw", x, s, t, part]
            if part == 0:
                copy(engine, live["dw_rows", x, s, t][:, 0:512], total[:])
            else:
                copy(engine, live["dw_rows", x, s, t][:, 512:768], total[:, 256:512])

        def dw_store(engine, x, s, t):
            view = out_1_by_head if x == "v" else out_1_by_four
            nc.sync.dma_start(out=view[2 * TENSORS.index(x) + int(s), int(t)], in_=live["dw_rows", x, s, t][:])

        def dx(engine, stage, g, form, n, members):
            for member in members.split(","):
                if member == STAGES[stage][0]:
                    total = sum_psum.tile([P, BANK], F32, tag="sum")
                    live["dx", stage, g, form, n] = total
                codes, scales = live["features", member[0] + g + member[1]]
                k = 2 * TENSORS.index(member[0]) + int(member[1])
                if form == "m":
                    cols = slice(P * int(n), P * int(n) + P)
                    lhs, lhs_scale = codes[:, cols].bitcast(E5M2), scales[:, cols]
                    rhs, rhs_scale = w_codes[:, k, 0:BANK].bitcast(E4M3), w_scales[:, k, 0:BANK]
                else:
                    cols = slice(BANK + P * int(n), BANK + P * int(n) + P)
                    lhs, lhs_scale = w_codes[:, k, cols].bitcast(E4M3), w_scales[:, k, cols]
                    rhs, rhs_scale = codes[:].bitcast(E5M2), scales[:]
                nc.tensor.matmul_mx(
                    out=live["dx", stage, g, form, n][:], lhsT=lhs, lhsT_scale=lhs_scale, rhs=rhs, rhs_scale=rhs_scale,
                    start=(member == STAGES[stage][0]), stop=(member == STAGES[stage][-1]),
                )

        def dx_rows(g, pair):
            if ("dx_rows", g, pair) not in live:
                rows = dx_pool.tile([P, 2, HID], F32)
                live["dx_rows", g, pair] = rows
            return live["dx_rows", g, pair]

        def dx_place(g, form, n):
            if form == "m":
                return dx_rows(g, int(n) // 2)[:, int(n) % 2, 0:BANK]
            if ("tail", g, n) not in live:
                tail = tail_pool.tile([P, BANK], F32)
                live["tail", g, n] = tail
            return live["tail", g, n][:]

        def dx_out(engine, g, form, n):
            copy(engine, dx_place(g, form, n), live["dx", "A", g, form, n][:])

        def dx_add(engine, g, form, n):
            place = dx_place(g, form, n)
            nc.vector.tensor_tensor(out=place, in0=live["dx", "B", g, form, n][:], in1=place, op=mybir.AluOpType.add)

        def dx_turn(engine, g, n):
            bank = turn_psum.tile([P, 4, P], F32, tag="turned")
            for j in range(4):
                nc.tensor.transpose(bank[:, j, :], live["tail", g, n][:, P * j:P * j + P], identity[:])
            live["tail_turned", g, n] = bank

        def dx_tail(engine, g, n, pair):
            start = BANK + P * int(n)
            j = 2 * int(pair)
            copy(engine, dx_rows(g, int(pair))[:, :, start:start + P], live["tail_turned", g, n][:, j:j + 2, :])

        def dx_store(engine, g, pair):
            j = 2 * int(pair)
            nc.sync.dma_start(out=out_0_rows[0, int(g), :, j:j + 2, :], in_=live["dx_rows", g, int(pair)][:])

        run = {
            "load": load, "group": group, "quant": quant, "table": table, "mult": mult, "add": add,
            "quant_tokens": quant_tokens, "turn": turn, "group_features": group_features, "quant_features": quant_features,
            "dw": dw, "dw_out": dw_out, "dw_store": dw_store,
            "dx": dx, "dx_out": dx_out, "dx_add": dx_add, "dx_turn": dx_turn, "dx_tail": dx_tail, "dx_store": dx_store,
        }
        for line in ORDER.split(";"):
            engine, name, *arguments = line.split()
            run[name](engine, *arguments)
